import numpy as np
import ml_dtypes


def mxq(x, axis, fmt="e4m3"):
    dtype, down = {"e4m3": (ml_dtypes.float8_e4m3fn, 7), "e5m2": (ml_dtypes.float8_e5m2, 14)}[fmt]
    v = np.moveaxis(np.asarray(x, np.float32).astype(ml_dtypes.bfloat16).astype(np.float64), axis, -1)
    blocks = v.reshape(v.shape[:-1] + (-1, 32))
    amax = np.abs(blocks).max(-1, keepdims=True)
    byte = np.maximum(np.where(amax > 0, np.frexp(amax)[1] - 1 + 127, 0) - down, 1)
    scale = np.exp2(byte - 127.0)
    codes = (blocks / scale).astype(np.float32).astype(dtype).astype(np.float64)
    return np.moveaxis((codes * scale).reshape(v.shape), -1, axis)


WIDE = False


def mx_kscale(k):
    if not WIDE:
        return np.ones(k)
    levels = np.array([20, -20, 10, -10, 0])
    a = np.random.permutation(np.resize(levels, k // 512 * 4)).reshape(k // 512, 4)
    idx = np.arange(k)
    return np.exp2(a[idx // 512, idx % 128 // 32])


BF16 = ml_dtypes.bfloat16


def bf(x):
    return np.asarray(x, np.float32).astype(BF16)


def f64(x):
    return np.asarray(x).astype(np.float64)


B, C_IN, C_OUT, H, W = 2, 384, 512, 64, 64
P = 4
G = P * P


def _to_groups(t):
    Bb, K, Hh, Ww = t.shape
    H4, W4 = Hh // P, Ww // P
    t = t.reshape(Bb, K, H4, P, W4, P).transpose(0, 2, 4, 3, 5, 1)
    return t.reshape(Bb * H4 * W4, G, K).transpose(1, 0, 2)


def _from_groups(t, Bb, Hh, Ww):
    H4, W4 = Hh // P, Ww // P
    K = t.shape[-1]
    t = t.transpose(1, 0, 2).reshape(Bb, H4, W4, P, P, K).transpose(0, 5, 1, 3, 2, 4)
    return t.reshape(Bb, K, Hh, Ww)


def setup_inputs():
    u = mx_kscale(C_OUT)
    bound = np.sqrt(6.0 / (C_IN + C_OUT))
    x = np.random.standard_normal((B, C_IN, H, W))
    Wg = np.random.uniform(-bound, bound, (G, C_OUT, C_IN)) / u[None, :, None]
    bg = np.random.standard_normal((G, C_OUT)) * 0.25
    g = np.random.standard_normal((B, C_OUT, H, W)) * np.exp2(np.random.randint(-12, 1, (B, 1, H, W))) * 8.0 * u[None, :, None, None]
    return {"x": bf(x), "Wg": bf(Wg), "bg": bf(bg), "grad_out": bf(g)}


def reference(x, Wg, bg, grad_out):
    Bb, O, Hh, Ww = grad_out.shape
    gq = mxq(f64(grad_out), 1, "e5m2")
    wq = mxq(f64(Wg), 1, "e4m3")
    gg = _to_groups(gq)
    gx = gg @ wq
    return _from_groups(gx, Bb, Hh, Ww)

@@ -1,0 +1,112 @@
+from contextlib import ExitStack
+
+import concourse.bass as bass
+import concourse.mybir as mybir
+import concourse.tile as tile
+
+FLOPS = 2 * 16 * 512 * 512 * 384
+BYTES = 2 * 512 * 4096 * 2 + 16 * 512 * 384 * 2 + 2 * 384 * 4096 * 4
+
+BF16 = mybir.dt.bfloat16
+F32 = mybir.dt.float32
+U32 = mybir.dt.uint32
+U8 = mybir.dt.uint8
+E4 = mybir.dt.float8_e4m3fn_x4
+E5 = mybir.dt.float8_e5m2_x4
+P = 128
+
+
+def tile_groupwiselinearprojector_t_kernel(tc, x, Wg, bg, grad_out, out):
+    nc = tc.nc
+    with ExitStack() as ctx:
+        keep = ctx.enter_context(tc.tile_pool(name="keep", bufs=1))
+        work = ctx.enter_context(tc.tile_pool(name="work", bufs=1))
+        psum = ctx.enter_context(tc.psum_pool(name="psum", bufs=8))
+
+        gc = keep.tile([P, 16, 512], U32, name="gc", align_bytes=64)
+        gs = keep.tile([P, 16, 512], U8, name="gs", align_bytes=64)
+        wc = keep.tile([P, 3, 16, 128], U32, name="wc", align_bytes=64)
+        ws = keep.tile([P, 3, 16, 128], U8, name="ws", align_bytes=64)
+
+        def copy_on(eng, dst, src):
+            if eng == "v":
+                nc.vector.tensor_copy(out=dst, in_=src)
+            else:
+                nc.scalar.copy(out=dst, in_=src)
+
+        rawg = {}
+        for b in range(2):
+            gv = grad_out[b].rearrange("(p j) r c -> p j (r c)", j=4)
+            for h in range(2):
+                t_ = work.tile([P, 4, 2048], BF16, name="rawg%d%d" % (b, h), tag="big", bufs=4)
+                nc.sync.dma_start(out=t_[:], in_=gv[:, :, 2048 * h : 2048 * h + 2048])
+                rawg[(b, h)] = t_
+        wv = Wg.rearrange("g (p j) c -> p g (j c)", j=4)
+        raww = {}
+        for s in range(4):
+            t_ = work.tile([P, 4, 1536], BF16, name="raww%d" % s, tag="raww", bufs=4)
+            nc.sync.dma_start(out=t_[:], in_=wv[:, 4 * s : 4 * s + 4, :])
+            raww[s] = t_
+
+        for b in range(2):
+            for h in range(2):
+                gus = []
+                for rm in range(4):
+                    gu = work.tile([P, 4, 128, 4], BF16, name="gu%d%d%d" % (b, h, rm), tag="grp", bufs=6, align_bytes=64)
+                    src = rawg[(b, h)][:].rearrange(
+                        "p t (r4 rm c4 cm) -> p rm r4 c4 t cm", r4=8, rm=4, c4=16, cm=4
+                    )[:, rm]
+                    dst = gu[:].rearrange("p cm (r4 c4) t -> p r4 c4 t cm", r4=8, c4=16)
+                    copy_on("v" if rm % 2 == 0 else "s", dst, src)
+                    gus.append(gu)
+                for rm in range(4):
+                    for cm in range(4):
+                        g = 4 * rm + cm
+                        lo = 256 * b + 128 * h
+                        nc.vector.quantize_mx(
+                            out=gc[:, g, lo : lo + 128].bitcast(E5),
+                            scales=gs[:, g, lo : lo + 128],
+                            in_=gus[rm][:, cm].rearrange("p x t -> p (x t)"),
+                        )
+
+        for t in range(3):
+            osb = []
+            for b in range(2):
+                osb.append(work.tile([P, 4096], F32, name="osb%d%d" % (t, b), tag="big", bufs=4))
+            for s in range(4):
+                wu = work.tile([P, 4, 128, 4], BF16, name="wu%d%d" % (s, t), tag="grp", bufs=6, align_bytes=64)
+                src = raww[s][:].rearrange("p g (j c) -> p g j c", j=4)[
+                    :, :, :, 128 * t : 128 * t + 128
+                ].rearrange("p g j (c i) -> p g c j i", i=4)
+                dst = wu[:].rearrange("p g (c i) j -> p g c j i", i=4)
+                copy_on("v" if t == 0 else "s", dst, src)
+                nc.vector.quantize_mx(
+                    out=wc[:, t, 4 * s : 4 * s + 4, :].rearrange("p g c -> p (g c)").bitcast(E4),
+                    scales=ws[:, t, 4 * s : 4 * s + 4, :].rearrange("p g c -> p (g c)"),
+                    in_=wu[:].rearrange("p g c j -> p (g c j)"),
+                )
+                ev = work.tile([P, 4, 512], F32, name="ev%d%d" % (t, s), tag="ev", bufs=3)
+                for cm in range(4):
+                    g = 4 * s + cm
+                    acc = psum.tile([P, 512], F32, name="acc%d_%d" % (t, g), tag="acc")
+                    nc.tensor.matmul_mx(
+                        out=acc[:],
+                        lhsT=wc[:, t, g, :].bitcast(E4),
+                        lhsT_scale=ws[:, t, g, :],
+                        rhs=gc[:, g, :].bitcast(E5),
+                        rhs_scale=gs[:, g, :],
+                        start=True,
+                        stop=True,
+                    )
+                    copy_on("v" if cm == 3 else "s", ev[:, cm, :], acc[:])
+                for b in range(2):
+                    dst = osb[b][:].rearrange(
+                        "p (r4 rm c4 cm) -> p rm r4 c4 cm", r4=16, rm=4, c4=16, cm=4
+                    )[:, s]
+                    src = ev[:, :, 256 * b : 256 * b + 256].rearrange(
+                        "p cm (r4 c4) -> p r4 c4 cm", r4=16, c4=16
+                    )
+                    nc.vector.tensor_copy(out=dst, in_=src)
+            for b in range(2):
+                ov = out[b].rearrange("(t p) r c -> t p (r c)", p=P)
+                nc.sync.dma_start(out=ov[t], in_=osb[b][:])

@@ -1,8 +1,6 @@
 from contextlib import ExitStack
 
-import concourse.bass as bass
 import concourse.mybir as mybir
-import concourse.tile as tile
 
 FLOPS = 2 * 16 * 512 * 512 * 384
 BYTES = 2 * 512 * 4096 * 2 + 16 * 512 * 384 * 2 + 2 * 384 * 4096 * 4
@@ -15,10 +13,23 @@ E4 = mybir.dt.float8_e4m3fn_x4
 E5 = mybir.dt.float8_e5m2_x4
 P = 128
 
+CHUNKS = ((0, 0, 4), (0, 4, 4), (0, 8, 4), (0, 12, 4), (1, 0, 8), (1, 8, 8))
+LOADS = (("g", 0), ("g", 1), ("g", 2), ("g", 3), ("g", 4), ("g", 5), ("w", 0), ("w", 1), ("w", 2), ("w", 3))
+PHASE1 = (("g", 0), ("g", 1), ("g", 2), ("g", 3), ("g", 4), ("g", 5), ("p", 0, 0))
+B01 = (0, 1)
+STEPS = [((1, 0), (0, 0, (0, 1))), ((2, 0), (0, 1, (0, 1))), ((3, 0), (0, 2, (0, 1))), ((0, 1), (0, 3, (0, 1))), ((1, 1), None), ((2, 1), (1, 0, (0,))), ((3, 1), (1, 1, (0,))), (None, (1, 2, (0,))), (None, (1, 3, (0,))), ((0, 2), (1, 0, (1,))), ((1, 2), (1, 1, (1,))), ((2, 2), (1, 2, (1,))), ((3, 2), (1, 3, (1,))), (None, (2, 0, (0,))), (None, (2, 1, (0,))), (None, (2, 2, (0,))), (None, (2, 3, (0,))), (None, (2, 0, (1,))), (None, (2, 1, (1,))), (None, (2, 2, (1,))), (None, (2, 3, (1,)))]
+MANUAL = True
+
+
+def v_evicts(t, s, bs):
+    return (3,) if s % 2 == 0 else ()
+
 
 def tile_groupwiselinearprojector_t_kernel(tc, x, Wg, bg, grad_out, out):
     nc = tc.nc
     with ExitStack() as ctx:
+        if MANUAL:
+            ctx.enter_context(tc.manual_schedule())
         keep = ctx.enter_context(tc.tile_pool(name="keep", bufs=1))
         work = ctx.enter_context(tc.tile_pool(name="work", bufs=1))
         psum = ctx.enter_context(tc.psum_pool(name="psum", bufs=8))
@@ -28,85 +39,155 @@ def tile_groupwiselinearprojector_t_kernel(tc, x, Wg, bg, grad_out, out):
         wc = keep.tile([P, 3, 16, 128], U32, name="wc", align_bytes=64)
         ws = keep.tile([P, 3, 16, 128], U8, name="ws", align_bytes=64)
 
-        def copy_on(eng, dst, src):
-            if eng == "v":
-                nc.vector.tensor_copy(out=dst, in_=src)
-            else:
-                nc.scalar.copy(out=dst, in_=src)
-
         rawg = {}
-        for b in range(2):
-            gv = grad_out[b].rearrange("(p j) r c -> p j (r c)", j=4)
-            for h in range(2):
-                t_ = work.tile([P, 4, 2048], BF16, name="rawg%d%d" % (b, h), tag="big", bufs=4)
-                nc.sync.dma_start(out=t_[:], in_=gv[:, :, 2048 * h : 2048 * h + 2048])
-                rawg[(b, h)] = t_
-        wv = Wg.rearrange("g (p j) c -> p g (j c)", j=4)
         raww = {}
-        for s in range(4):
-            t_ = work.tile([P, 4, 1536], BF16, name="raww%d" % s, tag="raww", bufs=4)
-            nc.sync.dma_start(out=t_[:], in_=wv[:, 4 * s : 4 * s + 4, :])
-            raww[s] = t_
+        gu = {}
+        wu = {}
+        acc = {}
+        ev = {}
+        osb = {}
+        wv = Wg.rearrange("g (p j) c -> p g (j c)", j=4)
 
-        for b in range(2):
-            for h in range(2):
-                gus = []
-                for rm in range(4):
-                    gu = work.tile([P, 4, 128, 4], BF16, name="gu%d%d%d" % (b, h, rm), tag="grp", bufs=6, align_bytes=64)
-                    src = rawg[(b, h)][:].rearrange(
-                        "p t (r4 rm c4 cm) -> p rm r4 c4 t cm", r4=8, rm=4, c4=16, cm=4
-                    )[:, rm]
-                    dst = gu[:].rearrange("p cm (r4 c4) t -> p r4 c4 t cm", r4=8, c4=16)
-                    copy_on("v" if rm % 2 == 0 else "s", dst, src)
-                    gus.append(gu)
-                for rm in range(4):
+        for kind, i in LOADS:
+            if kind == "g":
+                b, r0, n = CHUNKS[i]
+                rawg[i] = work.tile([P, 4, 256 * n], BF16, name="rawg%d" % i, tag="big", bufs=4)
+                gv = grad_out[b].rearrange("(p j) r c -> p j (r c)", j=4)
+                nc.sync.dma_start(out=rawg[i][:], in_=gv[:, :, 256 * r0 : 256 * (r0 + n)])
+            else:
+                raww[i] = work.tile([P, 4, 1536], BF16, name="raww%d" % i, tag="raww", bufs=4)
+                nc.sync.dma_start(out=raww[i][:], in_=wv[:, 4 * i : 4 * i + 4, :])
+
+        def regroup_g(ci):
+            b, r0, n = CHUNKS[ci]
+            src_all = rawg[ci][:].rearrange(
+                "p t (r4 rm c4 cm) -> p rm r4 c4 t cm", r4=n, rm=4, c4=16, cm=4
+            )
+            for e in range(2):
+                gu[(ci, e)] = work.tile(
+                    [P, 2, 4, 16 * n, 4], BF16, name="gu%d_%d" % (ci, e), tag="mid", bufs=4, align_bytes=64
+                )
+            for e in range(2):
+                for k in range(2):
+                    dst = gu[(ci, e)][:, k].rearrange("p cm (r4 c4) t -> p r4 c4 t cm", r4=n, c4=16)
+                    src = src_all[:, 2 * e + k]
+                    if e == 0:
+                        nc.vector.tensor_copy(out=dst, in_=src)
+                    else:
+                        nc.scalar.copy(out=dst, in_=src)
+
+        def quant_g(ci, e):
+            b, r0, n = CHUNKS[ci]
+            lo = 256 * b + 16 * r0
+            for e_ in (e,):
+                for k in range(2):
                     for cm in range(4):
-                        g = 4 * rm + cm
-                        lo = 256 * b + 128 * h
+                        g = 4 * (2 * e + k) + cm
                         nc.vector.quantize_mx(
-                            out=gc[:, g, lo : lo + 128].bitcast(E5),
-                            scales=gs[:, g, lo : lo + 128],
-                            in_=gus[rm][:, cm].rearrange("p x t -> p (x t)"),
+                            out=gc[:, g, lo : lo + 16 * n].bitcast(E5),
+                            scales=gs[:, g, lo : lo + 16 * n],
+                            in_=gu[(ci, e)][:, k, cm].rearrange("p x t -> p (x t)"),
                         )
 
-        for t in range(3):
-            osb = []
-            for b in range(2):
-                osb.append(work.tile([P, 4096], F32, name="osb%d%d" % (t, b), tag="big", bufs=4))
-            for s in range(4):
-                wu = work.tile([P, 4, 128, 4], BF16, name="wu%d%d" % (s, t), tag="grp", bufs=6, align_bytes=64)
-                src = raww[s][:].rearrange("p g (j c) -> p g j c", j=4)[
-                    :, :, :, 128 * t : 128 * t + 128
-                ].rearrange("p g j (c i) -> p g c j i", i=4)
-                dst = wu[:].rearrange("p g (c i) j -> p g c j i", i=4)
-                copy_on("v" if t == 0 else "s", dst, src)
-                nc.vector.quantize_mx(
-                    out=wc[:, t, 4 * s : 4 * s + 4, :].rearrange("p g c -> p (g c)").bitcast(E4),
-                    scales=ws[:, t, 4 * s : 4 * s + 4, :].rearrange("p g c -> p (g c)"),
-                    in_=wu[:].rearrange("p g c j -> p (g c j)"),
+        def regroup_w(s, t):
+            wu[(s, t)] = work.tile([P, 4, 128, 4], BF16, name="wu%d_%d" % (s, t), tag="wu", bufs=4, align_bytes=64)
+            src = raww[s][:].rearrange("p g (j c) -> p g j c", j=4)[
+                :, :, :, 128 * t : 128 * t + 128
+            ].rearrange("p g j (c i) -> p g c j i", i=4)
+            dst = wu[(s, t)][:].rearrange("p g (c i) j -> p g c j i", i=4)
+            nc.vector.tensor_copy(out=dst[:, 0:2], in_=src[:, 0:2])
+            nc.scalar.copy(out=dst[:, 2:4], in_=src[:, 2:4])
+
+        def quant_w(s, t):
+            nc.vector.quantize_mx(
+                out=wc[:, t, 4 * s : 4 * s + 4, :].rearrange("p g c -> p (g c)").bitcast(E4),
+                scales=ws[:, t, 4 * s : 4 * s + 4, :].rearrange("p g c -> p (g c)"),
+                in_=wu[(s, t)][:].rearrange("p g c j -> p (g c j)"),
+            )
+
+        def passes(o):
+            t, s, bs = o
+            if s == 0:
+                for b in bs:
+                    osb[(t, b)] = work.tile([P, 4096], F32, name="osb%d%d" % (t, b), tag="big", bufs=4)
+            for cm in range(4):
+                g = 4 * s + cm
+                a = psum.tile([P, 512], F32, name="acc%d_%d_%d" % (t, g, bs[0]), tag="acc")
+                nc.tensor.matmul_mx(
+                    out=a[:],
+                    lhsT=wc[:, t, g, :].bitcast(E4),
+                    lhsT_scale=ws[:, t, g, :],
+                    rhs=gc[:, g, :].bitcast(E5),
+                    rhs_scale=gs[:, g, :],
+                    start=True,
+                    stop=True,
                 )
-                ev = work.tile([P, 4, 512], F32, name="ev%d%d" % (t, s), tag="ev", bufs=3)
-                for cm in range(4):
-                    g = 4 * s + cm
-                    acc = psum.tile([P, 512], F32, name="acc%d_%d" % (t, g), tag="acc")
-                    nc.tensor.matmul_mx(
-                        out=acc[:],
-                        lhsT=wc[:, t, g, :].bitcast(E4),
-                        lhsT_scale=ws[:, t, g, :],
-                        rhs=gc[:, g, :].bitcast(E5),
-                        rhs_scale=gs[:, g, :],
-                        start=True,
-                        stop=True,
-                    )
-                    copy_on("v" if cm == 3 else "s", ev[:, cm, :], acc[:])
-                for b in range(2):
-                    dst = osb[b][:].rearrange(
-                        "p (r4 rm c4 cm) -> p rm r4 c4 cm", r4=16, rm=4, c4=16, cm=4
-                    )[:, s]
-                    src = ev[:, :, 256 * b : 256 * b + 256].rearrange(
-                        "p cm (r4 c4) -> p r4 c4 cm", r4=16, c4=16
-                    )
-                    nc.vector.tensor_copy(out=dst, in_=src)
-            for b in range(2):
-                ov = out[b].rearrange("(t p) r c -> t p (r c)", p=P)
-                nc.sync.dma_start(out=ov[t], in_=osb[b][:])
+                acc[(o, cm)] = a
+
+        def evict(o):
+            t, s, bs = o
+            lo = 256 * bs[0]
+            w = 256 * len(bs)
+            ev[o] = work.tile([P, 4, w], F32, name="ev%d_%d_%d" % (t, s, bs[0]), tag="mid", bufs=4, align_bytes=64)
+            on_v = v_evicts(t, s, bs)
+            for cm in on_v:
+                nc.vector.tensor_copy(out=ev[o][:, cm, :], in_=acc[(o, cm)][:, lo : lo + w])
+            for cm in range(4):
+                if cm not in on_v:
+                    nc.scalar.copy(out=ev[o][:, cm, :], in_=acc[(o, cm)][:, lo : lo + w])
+
+        def interleave(o):
+            t, s, bs = o
+            for i, b in enumerate(bs):
+                dst = osb[(t, b)][:].rearrange(
+                    "p (r4 rm c4 cm) -> p rm r4 c4 cm", r4=16, rm=4, c4=16, cm=4
+                )[:, s]
+                src = ev[o][:, :, 256 * i : 256 * i + 256].rearrange(
+                    "p cm (r4 c4) -> p r4 c4 cm", r4=16, c4=16
+                )
+                nc.vector.tensor_copy(out=dst, in_=src)
+                if s == 3:
+                    ov = out[b].rearrange("(t p) r c -> t p (r c)", p=P)
+                    nc.sync.dma_start(out=ov[t], in_=osb[(t, b)][:])
+
+        pend = None
+        for it in PHASE1:
+            if it[0] == "g":
+                regroup_g(it[1])
+                quant_g(it[1], 0)
+            else:
+                regroup_w(it[1], it[2])
+            if pend is not None:
+                if pend[0] == "g":
+                    quant_g(pend[1], 1)
+                else:
+                    quant_w(pend[1], pend[2])
+            pend = it
+        if pend[0] == "g":
+            quant_g(pend[1], 1)
+        else:
+            quant_w(pend[1], pend[2])
+
+        outs = [st[1] for st in STEPS if st[1] is not None]
+        issued = 0
+        prev = None
+        done_outs = 0
+        for p, o in STEPS:
+            if o is not None and issued == done_outs:
+                passes(o)
+                issued += 1
+            if p is not None:
+                regroup_w(p[0], p[1])
+            if o is not None:
+                evict(o)
+                done_outs += 1
+            if p is not None:
+                quant_w(p[0], p[1])
+            if issued == done_outs and issued < len(outs):
+                passes(outs[issued])
+                issued += 1
+            if prev is not None:
+                interleave(prev)
+            prev = o
+        if prev is not None:
+            interleave(prev)

@@ -22,7 +22,7 @@ MANUAL = True
 
 
 def v_evicts(t, s, bs):
-    return (3,) if s % 2 == 0 else ()
+    return (3,)
 
 
 def tile_groupwiselinearprojector_t_kernel(tc, x, Wg, bg, grad_out, out):
@@ -189,5 +189,8 @@ def tile_groupwiselinearprojector_t_kernel(tc, x, Wg, bg, grad_out, out):
             if prev is not None:
                 interleave(prev)
             prev = o
+            if o is not None and o[1] == 3:
+                interleave(o)
+                prev = None
         if prev is not None:
             interleave(prev)

@@ -22,7 +22,7 @@ MANUAL = True
 
 
 def v_evicts(t, s, bs):
-    return (3,)
+    return ()
 
 
 def tile_groupwiselinearprojector_t_kernel(tc, x, Wg, bg, grad_out, out):

@@ -7,6 +7,7 @@ BYTES = 2 * 512 * 4096 * 2 + 16 * 512 * 384 * 2 + 2 * 384 * 4096 * 4
 
 BF16 = mybir.dt.bfloat16
 F32 = mybir.dt.float32
+I32 = mybir.dt.int32
 U32 = mybir.dt.uint32
 U8 = mybir.dt.uint8
 E4 = mybir.dt.float8_e4m3fn_x4
@@ -14,30 +15,57 @@ E5 = mybir.dt.float8_e5m2_x4
 P = 128
 
 CHUNKS = ((0, 0, 4), (0, 4, 4), (0, 8, 4), (0, 12, 4), (1, 0, 8), (1, 8, 8))
-LOADS = (("g", 0), ("g", 1), ("g", 2), ("g", 3), ("g", 4), ("g", 5), ("w", 0), ("w", 1), ("w", 2), ("w", 3))
-PHASE1 = (("g", 0), ("g", 1), ("g", 2), ("g", 3), ("g", 4), ("g", 5), ("p", 0, 0))
-B01 = (0, 1)
-STEPS = [((1, 0), (0, 0, (0, 1))), ((2, 0), (0, 1, (0, 1))), ((3, 0), (0, 2, (0, 1))), ((0, 1), (0, 3, (0, 1))), ((1, 1), None), ((2, 1), (1, 0, (0,))), ((3, 1), (1, 1, (0,))), (None, (1, 2, (0,))), (None, (1, 3, (0,))), ((0, 2), (1, 0, (1,))), ((1, 2), (1, 1, (1,))), ((2, 2), (1, 2, (1,))), ((3, 2), (1, 3, (1,))), (None, (2, 0, (0,))), (None, (2, 1, (0,))), (None, (2, 2, (0,))), (None, (2, 3, (0,))), (None, (2, 0, (1,))), (None, (2, 1, (1,))), (None, (2, 2, (1,))), (None, (2, 3, (1,)))]
-MANUAL = True
+V_ROW_PHASES = (0, 1)
+LAG = 2
+AHEAD = 4
+PER_G = 2
+EZ_V_EVERY = 3
+UNIT = 640
 
 
-def v_evicts(t, s, bs):
+def v_evicts_j(t, s):
     return ()
 
 
 def tile_groupwiselinearprojector_t_kernel(tc, x, Wg, bg, grad_out, out):
     nc = tc.nc
     with ExitStack() as ctx:
-        if MANUAL:
-            ctx.enter_context(tc.manual_schedule())
+        ctx.enter_context(tc.manual_schedule())
         keep = ctx.enter_context(tc.tile_pool(name="keep", bufs=1))
         work = ctx.enter_context(tc.tile_pool(name="work", bufs=1))
         psum = ctx.enter_context(tc.psum_pool(name="psum", bufs=8))
 
-        gc = keep.tile([P, 16, 512], U32, name="gc", align_bytes=64)
-        gs = keep.tile([P, 16, 512], U8, name="gs", align_bytes=64)
+        g_a = keep.tile([P, 8 * UNIT], U32, name="g_a", align_bytes=64)
+        g_as = keep.tile([P, 8 * UNIT], U8, name="g_as", align_bytes=64)
+        g_b = keep.tile([P, 8 * UNIT + 128], U32, name="g_b", align_bytes=64)
+        g_bs = keep.tile([P, 8 * UNIT + 128], U8, name="g_bs", align_bytes=64)
+        g1c = keep.tile([P, 16, 256], U32, name="g1c", align_bytes=64)
+        g1s = keep.tile([P, 16, 256], U8, name="g1s", align_bytes=64)
         wc = keep.tile([P, 3, 16, 128], U32, name="wc", align_bytes=64)
         ws = keep.tile([P, 3, 16, 128], U8, name="ws", align_bytes=64)
+
+        def zpos(rm, q, cm):
+            base = UNIT * (2 * rm + q)
+            if cm == 0:
+                return g_a, g_as, base, base
+            if cm == 3:
+                return g_a, g_as, base + 512, base + 128
+            if cm == 1:
+                return g_b, g_bs, base + 128, base
+            return g_b, g_bs, base + 512, base + 256
+
+        def zero(tile_, words_per_unit, lo, hi):
+            v = tile_[:].bitcast(I32)[:, 0 : 8 * words_per_unit].rearrange("p (u w) -> p u w", w=words_per_unit)
+            nc.vector.memset(v[:, :, lo:hi], 0)
+
+        zero(g_a, UNIT, 128, 512)
+        zero(g_b, UNIT, 0, 128)
+        zero(g_b, UNIT, 256, 512)
+        nc.vector.memset(g_b[:].bitcast(I32)[:, 8 * UNIT : 8 * UNIT + 128], 0)
+        zero(g_as, UNIT // 4, 32, 128)
+        zero(g_bs, UNIT // 4, 0, 32)
+        zero(g_bs, UNIT // 4, 64, 128)
+        nc.vector.memset(g_bs[:].bitcast(I32)[:, 2 * UNIT : 2 * UNIT + 32], 0)
 
         rawg = {}
         raww = {}
@@ -46,51 +74,59 @@ def tile_groupwiselinearprojector_t_kernel(tc, x, Wg, bg, grad_out, out):
         acc = {}
         ev = {}
         osb = {}
+        oz = {}
         wv = Wg.rearrange("g (p j) c -> p g (j c)", j=4)
 
-        for kind, i in LOADS:
-            if kind == "g":
-                b, r0, n = CHUNKS[i]
-                rawg[i] = work.tile([P, 4, 256 * n], BF16, name="rawg%d" % i, tag="big", bufs=4)
-                gv = grad_out[b].rearrange("(p j) r c -> p j (r c)", j=4)
-                nc.sync.dma_start(out=rawg[i][:], in_=gv[:, :, 256 * r0 : 256 * (r0 + n)])
-            else:
-                raww[i] = work.tile([P, 4, 1536], BF16, name="raww%d" % i, tag="raww", bufs=4)
-                nc.sync.dma_start(out=raww[i][:], in_=wv[:, 4 * i : 4 * i + 4, :])
+        def load_g(i):
+            b, r0, n = CHUNKS[i]
+            rawg[i] = work.tile([P, 4, 256 * n], BF16, name="rawg%d" % i, tag="big", bufs=3)
+            gv = grad_out[b].rearrange("(p j) r c -> p j (r c)", j=4)
+            nc.sync.dma_start(out=rawg[i][:], in_=gv[:, :, 256 * r0 : 256 * (r0 + n)])
 
-        def regroup_g(ci):
+        def load_w(i):
+            raww[i] = work.tile([P, 4, 1536], BF16, name="raww%d" % i, tag="raww", bufs=3)
+            nc.sync.dma_start(out=raww[i][:], in_=wv[:, 4 * i : 4 * i + 4, :])
+
+        for i in range(4):
+            load_g(i)
+        for i in range(4):
+            load_w(i)
+        for i in range(4, 6):
+            load_g(i)
+
+        def regroup_g(ci, rm):
             b, r0, n = CHUNKS[ci]
-            src_all = rawg[ci][:].rearrange(
-                "p t (r4 rm c4 cm) -> p rm r4 c4 t cm", r4=n, rm=4, c4=16, cm=4
+            gu[(ci, rm)] = work.tile(
+                [P, 4, 16 * n, 4], BF16, name="gu%d_%d" % (ci, rm), tag="mid", bufs=6, align_bytes=64
             )
-            for e in range(2):
-                gu[(ci, e)] = work.tile(
-                    [P, 2, 4, 16 * n, 4], BF16, name="gu%d_%d" % (ci, e), tag="mid", bufs=4, align_bytes=64
-                )
-            for e in range(2):
-                for k in range(2):
-                    dst = gu[(ci, e)][:, k].rearrange("p cm (r4 c4) t -> p r4 c4 t cm", r4=n, c4=16)
-                    src = src_all[:, 2 * e + k]
-                    if e == 0:
-                        nc.vector.tensor_copy(out=dst, in_=src)
-                    else:
-                        nc.scalar.copy(out=dst, in_=src)
+            src = rawg[ci][:].rearrange("p t (r4 rm c4 cm) -> p rm r4 c4 t cm", r4=n, rm=4, c4=16, cm=4)[:, rm]
+            dst = gu[(ci, rm)][:].rearrange("p cm (r4 c4) t -> p r4 c4 t cm", r4=n, c4=16)
+            if rm in V_ROW_PHASES:
+                nc.vector.tensor_copy(out=dst, in_=src)
+            else:
+                nc.scalar.copy(out=dst, in_=src)
 
-        def quant_g(ci, e):
+        def quant_g(ci, rm):
             b, r0, n = CHUNKS[ci]
-            lo = 256 * b + 16 * r0
-            for e_ in (e,):
-                for k in range(2):
-                    for cm in range(4):
-                        g = 4 * (2 * e + k) + cm
-                        nc.vector.quantize_mx(
-                            out=gc[:, g, lo : lo + 16 * n].bitcast(E5),
-                            scales=gs[:, g, lo : lo + 16 * n],
-                            in_=gu[(ci, e)][:, k, cm].rearrange("p x t -> p (x t)"),
-                        )
+            for cm in range(4):
+                src = gu[(ci, rm)][:, cm].rearrange("p x t -> p (x t)")
+                if b == 0:
+                    codes, plane, blk, win = zpos(rm, r0 // 8, cm)
+                    lo = blk + 16 * (r0 % 8)
+                    nc.vector.quantize_mx(
+                        out=codes[:, lo : lo + 16 * n].bitcast(E5), scales=plane[:, lo : lo + 16 * n], in_=src
+                    )
+                else:
+                    g = 4 * rm + cm
+                    lo = 16 * r0
+                    nc.vector.quantize_mx(
+                        out=g1c[:, g, lo : lo + 16 * n].bitcast(E5), scales=g1s[:, g, lo : lo + 16 * n], in_=src
+                    )
 
         def regroup_w(s, t):
-            wu[(s, t)] = work.tile([P, 4, 128, 4], BF16, name="wu%d_%d" % (s, t), tag="wu", bufs=4, align_bytes=64)
+            wu[(s, t)] = work.tile(
+                [P, 4, 128, 4], BF16, name="wu%d_%d" % (s, t), tag="mid", bufs=6, align_bytes=64
+            )
             src = raww[s][:].rearrange("p g (j c) -> p g j c", j=4)[
                 :, :, :, 128 * t : 128 * t + 128
             ].rearrange("p g j (c i) -> p g c j i", i=4)
@@ -105,92 +141,144 @@ def tile_groupwiselinearprojector_t_kernel(tc, x, Wg, bg, grad_out, out):
                 in_=wu[(s, t)][:].rearrange("p g c j -> p (g c j)"),
             )
 
-        def passes(o):
-            t, s, bs = o
-            if s == 0:
-                for b in bs:
-                    osb[(t, b)] = work.tile([P, 4096], F32, name="osb%d%d" % (t, b), tag="big", bufs=4)
+        def passes_z(t, s, q):
+            a = psum.tile([P, 512], F32, name="az%d_%d_%d" % (t, s, q), tag="acc")
             for cm in range(4):
+                codes, plane, blk, win = zpos(s, q, cm)
                 g = 4 * s + cm
-                a = psum.tile([P, 512], F32, name="acc%d_%d_%d" % (t, g, bs[0]), tag="acc")
                 nc.tensor.matmul_mx(
                     out=a[:],
                     lhsT=wc[:, t, g, :].bitcast(E4),
                     lhsT_scale=ws[:, t, g, :],
-                    rhs=gc[:, g, :].bitcast(E5),
-                    rhs_scale=gs[:, g, :],
+                    rhs=codes[:, win : win + 512].bitcast(E5),
+                    rhs_scale=plane[:, win : win + 512],
+                    start=(cm == 0),
+                    stop=(cm == 3),
+                )
+            acc[("z", t, s, q)] = a
+
+        def evict_z(t, s, q, on_v):
+            dst = oz[(t, q)][:].rearrange("p (r4 rm c4 cm) -> p rm r4 c4 cm", r4=8, rm=4, c4=16, cm=4)[:, s]
+            src = acc[("z", t, s, q)][:].rearrange("p (cm r4 c4) -> p r4 c4 cm", cm=4, r4=8, c4=16)
+            if on_v:
+                nc.vector.tensor_copy(out=dst, in_=src)
+            else:
+                nc.scalar.copy(out=dst, in_=src)
+            if s == 3:
+                ov = out[0].rearrange("(t p) r c -> t p (r c)", p=P)
+                nc.sync.dma_start(out=ov[t][:, 2048 * q : 2048 * q + 2048], in_=oz[(t, q)][:])
+
+        def passes_j(t, s):
+            for cm in range(4):
+                g = 4 * s + cm
+                g0 = 4 * s + 2 * (cm // 2)
+                a = psum.tile([P, 512], F32, name="aj%d_%d" % (t, g), tag="acc")
+                nc.tensor.matmul_mx(
+                    out=a[:],
+                    lhsT=wc[:, t, g, :].bitcast(E4),
+                    lhsT_scale=ws[:, t, g, :],
+                    rhs=g1c[:, g0 : g0 + 2, :].rearrange("p g x -> p (g x)").bitcast(E5),
+                    rhs_scale=g1s[:, g0 : g0 + 2, :].rearrange("p g x -> p (g x)"),
                     start=True,
                     stop=True,
                 )
-                acc[(o, cm)] = a
+                acc[("j", t, s, cm)] = a
 
-        def evict(o):
-            t, s, bs = o
-            lo = 256 * bs[0]
-            w = 256 * len(bs)
-            ev[o] = work.tile([P, 4, w], F32, name="ev%d_%d_%d" % (t, s, bs[0]), tag="mid", bufs=4, align_bytes=64)
-            on_v = v_evicts(t, s, bs)
+        def evict_j(t, s):
+            ev[(t, s)] = work.tile([P, 4, 256], F32, name="ev%d_%d" % (t, s), tag="mid", bufs=6, align_bytes=64)
+            on_v = v_evicts_j(t, s)
             for cm in on_v:
-                nc.vector.tensor_copy(out=ev[o][:, cm, :], in_=acc[(o, cm)][:, lo : lo + w])
+                lo = 256 * (cm % 2)
+                nc.vector.tensor_copy(out=ev[(t, s)][:, cm, :], in_=acc[("j", t, s, cm)][:, lo : lo + 256])
             for cm in range(4):
                 if cm not in on_v:
-                    nc.scalar.copy(out=ev[o][:, cm, :], in_=acc[(o, cm)][:, lo : lo + w])
+                    lo = 256 * (cm % 2)
+                    nc.scalar.copy(out=ev[(t, s)][:, cm, :], in_=acc[("j", t, s, cm)][:, lo : lo + 256])
 
-        def interleave(o):
-            t, s, bs = o
-            for i, b in enumerate(bs):
-                dst = osb[(t, b)][:].rearrange(
-                    "p (r4 rm c4 cm) -> p rm r4 c4 cm", r4=16, rm=4, c4=16, cm=4
-                )[:, s]
-                src = ev[o][:, :, 256 * i : 256 * i + 256].rearrange(
-                    "p cm (r4 c4) -> p r4 c4 cm", r4=16, c4=16
-                )
-                nc.vector.tensor_copy(out=dst, in_=src)
-                if s == 3:
-                    ov = out[b].rearrange("(t p) r c -> t p (r c)", p=P)
-                    nc.sync.dma_start(out=ov[t], in_=osb[(t, b)][:])
+        def interleave_j(t, s):
+            dst = osb[t][:].rearrange("p (r4 rm c4 cm) -> p rm r4 c4 cm", r4=16, rm=4, c4=16, cm=4)[:, s]
+            src = ev[(t, s)][:].rearrange("p cm (r4 c4) -> p r4 c4 cm", r4=16, c4=16)
+            nc.vector.tensor_copy(out=dst, in_=src)
+            if s == 3:
+                ov = out[1].rearrange("(t p) r c -> t p (r c)", p=P)
+                nc.sync.dma_start(out=ov[t], in_=osb[t][:])
 
-        pend = None
-        for it in PHASE1:
-            if it[0] == "g":
-                regroup_g(it[1])
-                quant_g(it[1], 0)
-            else:
-                regroup_w(it[1], it[2])
-            if pend is not None:
-                if pend[0] == "g":
-                    quant_g(pend[1], 1)
-                else:
-                    quant_w(pend[1], pend[2])
-            pend = it
-        if pend[0] == "g":
-            quant_g(pend[1], 1)
-        else:
-            quant_w(pend[1], pend[2])
+        ezq = []
+        state = {"ez": 0, "z1": 0, "head": 0, "pend": []}
+        z1 = [(t, s, 1) for t in range(3) for s in range(4)]
 
-        outs = [st[1] for st in STEPS if st[1] is not None]
-        issued = 0
+        def flush():
+            for ci, rm in state["pend"]:
+                quant_g(ci, rm)
+            state["pend"] = []
+
+        def pop_ez(k):
+            for i in range(k):
+                if state["head"] < len(ezq):
+                    t, s, q = ezq[state["head"]]
+                    state["head"] = state["head"] + 1
+                    evict_z(t, s, q, state["ez"] % EZ_V_EVERY == EZ_V_EVERY - 1)
+                    state["ez"] = state["ez"] + 1
+
+        def issue(k):
+            for i in range(k):
+                if state["z1"] < len(z1):
+                    t, s, q = z1[state["z1"]]
+                    state["z1"] = state["z1"] + 1
+                    if s == 0:
+                        oz[(t, q)] = work.tile([P, 2048], F32, name="oz%d_%d" % (t, q), tag="oz", bufs=3)
+                    passes_z(t, s, q)
+                    ezq.append((t, s, q))
+
+        def do_g(ci, mid_work):
+            for rm in range(4):
+                regroup_g(ci, rm)
+            if mid_work:
+                pop_ez(PER_G)
+                issue(PER_G)
+            for rm in V_ROW_PHASES:
+                quant_g(ci, rm)
+            flush()
+            for rm in range(4):
+                if rm not in V_ROW_PHASES:
+                    state["pend"] = state["pend"] + [(ci, rm)]
+
+        for ci in range(4):
+            do_g(ci, False)
+        flush()
+        for t in range(3):
+            oz[(t, 0)] = work.tile([P, 2048], F32, name="oz%d_0" % t, tag="oz", bufs=3)
+        for s in range(4):
+            for t in range(3):
+                regroup_w(s, t)
+                if len(ezq) - state["head"] >= LAG:
+                    pop_ez(1)
+                quant_w(s, t)
+                passes_z(t, s, 0)
+                ezq.append((t, s, 0))
+        issue(AHEAD)
+        for ci in range(4, 6):
+            do_g(ci, True)
+            pop_ez(PER_G)
+            issue(PER_G)
+        flush()
+        while state["head"] < len(ezq) or state["z1"] < len(z1):
+            pop_ez(1)
+            issue(1)
+
+        stages = [(t, s) for t in range(3) for s in range(4)]
         prev = None
-        done_outs = 0
-        for p, o in STEPS:
-            if o is not None and issued == done_outs:
-                passes(o)
-                issued += 1
-            if p is not None:
-                regroup_w(p[0], p[1])
-            if o is not None:
-                evict(o)
-                done_outs += 1
-            if p is not None:
-                quant_w(p[0], p[1])
-            if issued == done_outs and issued < len(outs):
-                passes(outs[issued])
-                issued += 1
+        for i, (t, s) in enumerate(stages):
+            if s == 0:
+                osb[t] = work.tile([P, 4096], F32, name="osb%d" % t, tag="big", bufs=3)
+            if i == 0:
+                passes_j(t, s)
+            evict_j(t, s)
+            if i + 1 < len(stages):
+                passes_j(stages[i + 1][0], stages[i + 1][1])
             if prev is not None:
-                interleave(prev)
-            prev = o
-            if o is not None and o[1] == 3:
-                interleave(o)
+                interleave_j(prev[0], prev[1])
+            prev = (t, s)
+            if s == 3:
+                interleave_j(t, s)
                 prev = None
-        if prev is not None:
-            interleave(prev)

@@ -16,7 +16,7 @@ P = 128
 
 CHUNKS = ((0, 0, 4), (0, 4, 4), (0, 8, 4), (0, 12, 4), (1, 0, 8), (1, 8, 8))
 V_ROW_PHASES = (0, 1)
-LAG = 2
+LAG = 3
 AHEAD = 4
 PER_G = 2
 EZ_V_EVERY = 3
@@ -87,11 +87,11 @@ def tile_groupwiselinearprojector_t_kernel(tc, x, Wg, bg, grad_out, out):
             raww[i] = work.tile([P, 4, 1536], BF16, name="raww%d" % i, tag="raww", bufs=3)
             nc.sync.dma_start(out=raww[i][:], in_=wv[:, 4 * i : 4 * i + 4, :])
 
-        for i in range(4):
+        for i in range(2):
             load_g(i)
         for i in range(4):
             load_w(i)
-        for i in range(4, 6):
+        for i in range(2, 6):
             load_g(i)
 
         def regroup_g(ci, rm):
@@ -204,7 +204,7 @@ def tile_groupwiselinearprojector_t_kernel(tc, x, Wg, bg, grad_out, out):
                 nc.sync.dma_start(out=ov[t], in_=osb[t][:])
 
         ezq = []
-        state = {"ez": 0, "z1": 0, "head": 0, "pend": []}
+        state = {"ez": 0, "z1": 0, "head": 0, "pend": [], "open": False, "w": None}
         z1 = [(t, s, 1) for t in range(3) for s in range(4)]
 
         def flush():
@@ -222,7 +222,7 @@ def tile_groupwiselinearprojector_t_kernel(tc, x, Wg, bg, grad_out, out):
 
         def issue(k):
             for i in range(k):
-                if state["z1"] < len(z1):
+                if state["open"] and state["z1"] < len(z1):
                     t, s, q = z1[state["z1"]]
                     state["z1"] = state["z1"] + 1
                     if s == 0:
@@ -230,9 +230,18 @@ def tile_groupwiselinearprojector_t_kernel(tc, x, Wg, bg, grad_out, out):
                     passes_z(t, s, q)
                     ezq.append((t, s, q))
 
+        def finish_w():
+            if state["w"] is not None:
+                s_, t_ = state["w"]
+                quant_w(s_, t_)
+                passes_z(t_, s_, 0)
+                ezq.append((t_, s_, 0))
+                state["w"] = None
+
         def do_g(ci, mid_work):
             for rm in range(4):
                 regroup_g(ci, rm)
+            finish_w()
             if mid_work:
                 pop_ez(PER_G)
                 issue(PER_G)
@@ -243,7 +252,7 @@ def tile_groupwiselinearprojector_t_kernel(tc, x, Wg, bg, grad_out, out):
                 if rm not in V_ROW_PHASES:
                     state["pend"] = state["pend"] + [(ci, rm)]
 
-        for ci in range(4):
+        for ci in range(2):
             do_g(ci, False)
         flush()
         for t in range(3):
@@ -253,9 +262,13 @@ def tile_groupwiselinearprojector_t_kernel(tc, x, Wg, bg, grad_out, out):
                 regroup_w(s, t)
                 if len(ezq) - state["head"] >= LAG:
                     pop_ez(1)
-                quant_w(s, t)
-                passes_z(t, s, 0)
-                ezq.append((t, s, 0))
+                finish_w()
+                state["w"] = (s, t)
+        for ci in range(2, 4):
+            do_g(ci, True)
+            pop_ez(PER_G)
+        flush()
+        state["open"] = True
         issue(AHEAD)
         for ci in range(4, 6):
             do_g(ci, True)

@@ -19,7 +19,7 @@ V_ROW_PHASES = (0, 1)
 LAG = 3
 AHEAD = 4
 PER_G = 2
-EZ_V_EVERY = 3
+EZ_V_EVERY = 6
 UNIT = 640
 
 

@@ -14,12 +14,12 @@ E4 = mybir.dt.float8_e4m3fn_x4
 E5 = mybir.dt.float8_e5m2_x4
 P = 128
 
-CHUNKS = ((0, 0, 4), (0, 4, 4), (0, 8, 4), (0, 12, 4), (1, 0, 8), (1, 8, 8))
+CHUNKS = ((0, 0, 4), (0, 4, 4), (0, 8, 8), (1, 0, 8), (1, 8, 8))
 V_ROW_PHASES = (0, 1)
 LAG = 3
 AHEAD = 4
 PER_G = 2
-EZ_V_EVERY = 6
+EZ_V_EVERY = 3
 UNIT = 640
 
 
@@ -91,7 +91,7 @@ def tile_groupwiselinearprojector_t_kernel(tc, x, Wg, bg, grad_out, out):
             load_g(i)
         for i in range(4):
             load_w(i)
-        for i in range(2, 6):
+        for i in range(2, 5):
             load_g(i)
 
         def regroup_g(ci, rm):
@@ -264,13 +264,13 @@ def tile_groupwiselinearprojector_t_kernel(tc, x, Wg, bg, grad_out, out):
                     pop_ez(1)
                 finish_w()
                 state["w"] = (s, t)
-        for ci in range(2, 4):
+        for ci in range(2, 3):
             do_g(ci, True)
             pop_ez(PER_G)
         flush()
         state["open"] = True
         issue(AHEAD)
-        for ci in range(4, 6):
+        for ci in range(3, 5):
             do_g(ci, True)
             pop_ez(PER_G)
             issue(PER_G)

@@ -13,18 +13,85 @@ U8 = mybir.dt.uint8
 E4 = mybir.dt.float8_e4m3fn_x4
 E5 = mybir.dt.float8_e5m2_x4
 P = 128
-
-CHUNKS = ((0, 0, 4), (0, 4, 4), (0, 8, 8), (1, 0, 8), (1, 8, 8))
-V_ROW_PHASES = (0, 1)
-LAG = 3
-AHEAD = 4
-PER_G = 2
-EZ_V_EVERY = 3
 UNIT = 640
 
+PIECES = {0: ((0, 1), (1, 1), (2, 2), (4, 2), (6, 2)), 1: ((0, 8),), 2: ((0, 8),), 3: ((0, 8),)}
+WPIECES = {0: ((0, 2), (2, 4)), 1: ((0, 4),), 2: ((0, 4),), 3: ((0, 4),)}
+A_V = (0, 1)
+V3 = "rgB0 rgB1 qzB0 qzB1 qzB2 qzB3 rgC0 rgD0 rgD1 qj0 rgC2 rgD2 qj1 rgD3 qj2 qj3"
+S3 = "rgB2 rgB3 ezA ezA ezA rgC1 ez ez ez ez rgC3 ez ez ez ez ez ez ez ez"
+EJ_V = ((0, 3), (1, 3))
 
-def v_evicts_j(t, s):
-    return ()
+
+def SCRIPTS(units, stages):
+    V, S, PE, SP = [], [], [], []
+    for h in range(len(PIECES[0])):
+        SP.append(("ld", 0, h))
+    for s in range(4):
+        for h in range(len(WPIECES[s])):
+            SP.append(("ldw", s, h))
+    for c in (1, 2, 3):
+        SP.append(("ld", c, 0))
+    for q in range(2):
+        for t in range(3):
+            SP.append(("sz", q, t))
+    for t in range(3):
+        SP.append(("sj", t))
+    for s, t in units:
+        PE.append(("pz", 0, t, s))
+    zb = [(t, s) for t in range(3) for s in range(4)]
+    for t, s in zb:
+        PE.append(("pz", 1, t, s))
+    for t, s in stages:
+        PE.append(("pj", t, s))
+    V.append(("zero",))
+    for h in range(len(PIECES[0])):
+        for rm in range(4):
+            (V if rm in A_V else S).append(("rg", 0, rm, h))
+    V.append(("qz", 0, 0))
+    V.append(("qz", 0, 1))
+    for s in range(4):
+        for h in range(len(WPIECES[s])):
+            V.append(("rw", s, 0, h))
+            if s == 0 and h == 0:
+                V.append(("qz", 0, 2))
+        for h in range(len(WPIECES[s])):
+            V.append(("rw", s, 1, h))
+            S.append(("rw", s, 2, h))
+        V.append(("qw", s, 0))
+        if s == 0:
+            V.append(("qz", 0, 3))
+        V.append(("qw", s, 1))
+        V.append(("qw", s, 2))
+        if s >= 1:
+            for t in range(3):
+                S.append(("ez", 0, t, s - 1))
+    cn = {"B": 1, "C": 2, "D": 3}
+    na = [9]
+    nb = [0]
+    for eng, txt in ((V, V3), (S, S3)):
+        for w in txt.split():
+            if w.startswith("rg"):
+                eng.append(("rg", cn[w[2]], int(w[3]), 0))
+            elif w.startswith("qz"):
+                eng.append(("qz", 1, int(w[3])))
+            elif w.startswith("qj"):
+                eng.append(("qj", int(w[2])))
+            elif w == "ezA":
+                s_, t_ = units[na[0]]
+                na[0] = na[0] + 1
+                eng.append(("ez", 0, t_, s_))
+            elif w == "ez":
+                t_, s_ = zb[nb[0]]
+                nb[0] = nb[0] + 1
+                eng.append(("ez", 1, t_, s_))
+    for i, (t, s) in enumerate(stages):
+        for cm in range(4):
+            (V if (i % 2, cm) in EJ_V else S).append(("ej", t, s, cm))
+        if i >= 1:
+            V.append(("ij",) + stages[i - 1])
+    V.append(("ij", 2, 3))
+    return {"SP": SP, "V": V, "S": S, "PE": PE}
 
 
 def tile_groupwiselinearprojector_t_kernel(tc, x, Wg, bg, grad_out, out):
@@ -35,17 +102,25 @@ def tile_groupwiselinearprojector_t_kernel(tc, x, Wg, bg, grad_out, out):
         work = ctx.enter_context(tc.tile_pool(name="work", bufs=1))
         psum = ctx.enter_context(tc.psum_pool(name="psum", bufs=8))
 
-        g_a = keep.tile([P, 8 * UNIT], U32, name="g_a", align_bytes=64)
-        g_as = keep.tile([P, 8 * UNIT], U8, name="g_as", align_bytes=64)
-        g_b = keep.tile([P, 8 * UNIT + 128], U32, name="g_b", align_bytes=64)
-        g_bs = keep.tile([P, 8 * UNIT + 128], U8, name="g_bs", align_bytes=64)
+        g_a = keep.tile([P, 4 * UNIT], U32, name="g_a", align_bytes=64)
+        g_as = keep.tile([P, 4 * UNIT], U8, name="g_as", align_bytes=64)
+        g_b = keep.tile([P, 4 * UNIT + 128], U32, name="g_b", align_bytes=64)
+        g_bs = keep.tile([P, 4 * UNIT + 128], U8, name="g_bs", align_bytes=64)
         g1c = keep.tile([P, 16, 256], U32, name="g1c", align_bytes=64)
         g1s = keep.tile([P, 16, 256], U8, name="g1s", align_bytes=64)
         wc = keep.tile([P, 3, 16, 128], U32, name="wc", align_bytes=64)
         ws = keep.tile([P, 3, 16, 128], U8, name="ws", align_bytes=64)
 
+        tiles = {}
+        queues = {"V": [], "S": [], "PE": [], "SP": []}
+        ops = {}
+
+        def op(eng, key, deps, fn):
+            queues[eng].append(key)
+            ops[key] = (deps, fn)
+
         def zpos(rm, q, cm):
-            base = UNIT * (2 * rm + q)
+            base = UNIT * rm
             if cm == 0:
                 return g_a, g_as, base, base
             if cm == 3:
@@ -55,93 +130,94 @@ def tile_groupwiselinearprojector_t_kernel(tc, x, Wg, bg, grad_out, out):
             return g_b, g_bs, base + 512, base + 256
 
         def zero(tile_, words_per_unit, lo, hi):
-            v = tile_[:].bitcast(I32)[:, 0 : 8 * words_per_unit].rearrange("p (u w) -> p u w", w=words_per_unit)
+            v = tile_[:].bitcast(I32)[:, 0 : 4 * words_per_unit].rearrange("p (u w) -> p u w", w=words_per_unit)
             nc.vector.memset(v[:, :, lo:hi], 0)
 
-        zero(g_a, UNIT, 128, 512)
-        zero(g_b, UNIT, 0, 128)
-        zero(g_b, UNIT, 256, 512)
-        nc.vector.memset(g_b[:].bitcast(I32)[:, 8 * UNIT : 8 * UNIT + 128], 0)
-        zero(g_as, UNIT // 4, 32, 128)
-        zero(g_bs, UNIT // 4, 0, 32)
-        zero(g_bs, UNIT // 4, 64, 128)
-        nc.vector.memset(g_bs[:].bitcast(I32)[:, 2 * UNIT : 2 * UNIT + 32], 0)
+        def zeros():
+            zero(g_a, UNIT, 128, 512)
+            zero(g_b, UNIT, 0, 128)
+            zero(g_b, UNIT, 256, 512)
+            nc.vector.memset(g_b[:].bitcast(I32)[:, 4 * UNIT : 4 * UNIT + 128], 0)
+            zero(g_as, UNIT // 4, 32, 128)
+            zero(g_bs, UNIT // 4, 0, 32)
+            zero(g_bs, UNIT // 4, 64, 128)
+            nc.vector.memset(g_bs[:].bitcast(I32)[:, UNIT : UNIT + 32], 0)
 
-        rawg = {}
-        raww = {}
-        gu = {}
-        wu = {}
-        acc = {}
-        ev = {}
-        osb = {}
-        oz = {}
         wv = Wg.rearrange("g (p j) c -> p g (j c)", j=4)
 
-        def load_g(i):
-            b, r0, n = CHUNKS[i]
-            rawg[i] = work.tile([P, 4, 256 * n], BF16, name="rawg%d" % i, tag="big", bufs=3)
-            gv = grad_out[b].rearrange("(p j) r c -> p j (r c)", j=4)
-            nc.sync.dma_start(out=rawg[i][:], in_=gv[:, :, 256 * r0 : 256 * (r0 + n)])
+        def raw_tile(c):
+            if ("raw", c) not in tiles:
+                tiles[("raw", c)] = work.tile([P, 4, 2048], BF16, name="rawg%d" % c, tag="big", bufs=3)
+            return tiles[("raw", c)]
 
-        def load_w(i):
-            raww[i] = work.tile([P, 4, 1536], BF16, name="raww%d" % i, tag="raww", bufs=3)
-            nc.sync.dma_start(out=raww[i][:], in_=wv[:, 4 * i : 4 * i + 4, :])
+        def load_g(c, lo, hi):
+            gv = grad_out[c // 2].rearrange("(p j) r c -> p j (r c)", j=4)
+            o = 2048 * (c % 2)
+            nc.sync.dma_start(out=raw_tile(c)[:, :, lo:hi], in_=gv[:, :, o + lo : o + hi])
 
-        for i in range(2):
-            load_g(i)
-        for i in range(4):
-            load_w(i)
-        for i in range(2, 5):
-            load_g(i)
+        def load_w(s, g0, g1):
+            if ("raww", s) not in tiles:
+                tiles[("raww", s)] = work.tile([P, 4, 1536], BF16, name="raww%d" % s, tag="raww", bufs=4, align_bytes=64)
+            nc.sync.dma_start(out=tiles[("raww", s)][:, g0:g1, :], in_=wv[:, 4 * s + g0 : 4 * s + g1, :])
 
-        def regroup_g(ci, rm):
-            b, r0, n = CHUNKS[ci]
-            gu[(ci, rm)] = work.tile(
-                [P, 4, 16 * n, 4], BF16, name="gu%d_%d" % (ci, rm), tag="mid", bufs=6, align_bytes=64
-            )
-            src = rawg[ci][:].rearrange("p t (r4 rm c4 cm) -> p rm r4 c4 t cm", r4=n, rm=4, c4=16, cm=4)[:, rm]
-            dst = gu[(ci, rm)][:].rearrange("p cm (r4 c4) t -> p r4 c4 t cm", r4=n, c4=16)
-            if rm in V_ROW_PHASES:
+        def gu_tile(c, rm):
+            k = ("gu", c, rm) if c < 2 else ("gu", 2, rm)
+            if k not in tiles:
+                if c < 2:
+                    tiles[k] = work.tile([P, 4, 128, 4], BF16, name="gu%d_%d" % (c, rm), tag="gu", bufs=4, align_bytes=64)
+                else:
+                    tiles[k] = work.tile([P, 4, 256, 4], BF16, name="gj_%d" % rm, tag="raww", bufs=4, align_bytes=64)
+            return tiles[k]
+
+        def regroup_g(eng, c, rm, r0, n):
+            src = raw_tile(c)[:].rearrange("p t (r4 rm c4 cm) -> p rm r4 c4 t cm", r4=8, rm=4, c4=16, cm=4)[:, rm, r0 : r0 + n]
+            o = 0 if c < 3 else 8
+            dst = gu_tile(c, rm)[:].rearrange("p cm (r4 c4) t -> p r4 c4 t cm", c4=16)[:, o + r0 : o + r0 + n]
+            if eng == "V":
                 nc.vector.tensor_copy(out=dst, in_=src)
             else:
                 nc.scalar.copy(out=dst, in_=src)
 
-        def quant_g(ci, rm):
-            b, r0, n = CHUNKS[ci]
+        def quant_z(q, rm):
             for cm in range(4):
-                src = gu[(ci, rm)][:, cm].rearrange("p x t -> p (x t)")
-                if b == 0:
-                    codes, plane, blk, win = zpos(rm, r0 // 8, cm)
-                    lo = blk + 16 * (r0 % 8)
-                    nc.vector.quantize_mx(
-                        out=codes[:, lo : lo + 16 * n].bitcast(E5), scales=plane[:, lo : lo + 16 * n], in_=src
-                    )
-                else:
-                    g = 4 * rm + cm
-                    lo = 16 * r0
-                    nc.vector.quantize_mx(
-                        out=g1c[:, g, lo : lo + 16 * n].bitcast(E5), scales=g1s[:, g, lo : lo + 16 * n], in_=src
-                    )
+                codes, plane, blk, win = zpos(rm, q, cm)
+                nc.vector.quantize_mx(
+                    out=codes[:, blk : blk + 128].bitcast(E5),
+                    scales=plane[:, blk : blk + 128],
+                    in_=gu_tile(q, rm)[:, cm].rearrange("p x t -> p (x t)"),
+                )
 
-        def regroup_w(s, t):
-            wu[(s, t)] = work.tile(
-                [P, 4, 128, 4], BF16, name="wu%d_%d" % (s, t), tag="mid", bufs=6, align_bytes=64
+        def quant_j(rm):
+            nc.vector.quantize_mx(
+                out=g1c[:, 4 * rm : 4 * rm + 4, :].rearrange("p g x -> p (g x)").bitcast(E5),
+                scales=g1s[:, 4 * rm : 4 * rm + 4, :].rearrange("p g x -> p (g x)"),
+                in_=gu_tile(2, rm)[:].rearrange("p g x t -> p (g x t)"),
             )
-            src = raww[s][:].rearrange("p g (j c) -> p g j c", j=4)[
-                :, :, :, 128 * t : 128 * t + 128
+
+        def regroup_w(eng, s, t, g0, g1):
+            k = ("wu", s, t)
+            if k not in tiles:
+                if eng == "V":
+                    tiles[k] = work.tile([P, 4, 128, 4], BF16, name="wu%d_%d" % (s, t), tag="wv", bufs=3, align_bytes=64)
+                else:
+                    tiles[k] = work.tile([P, 4, 128, 4], BF16, name="wu%d_%d" % (s, t), tag="wq", bufs=2, align_bytes=64)
+            src = tiles[("raww", s)][:].rearrange("p g (j c) -> p g j c", j=4)[
+                :, g0:g1, :, 128 * t : 128 * t + 128
             ].rearrange("p g j (c i) -> p g c j i", i=4)
-            dst = wu[(s, t)][:].rearrange("p g (c i) j -> p g c j i", i=4)
-            nc.vector.tensor_copy(out=dst[:, 0:2], in_=src[:, 0:2])
-            nc.scalar.copy(out=dst[:, 2:4], in_=src[:, 2:4])
+            dst = tiles[k][:].rearrange("p g (c i) j -> p g c j i", i=4)[:, g0:g1]
+            if eng == "V":
+                nc.vector.tensor_copy(out=dst, in_=src)
+            else:
+                nc.scalar.copy(out=dst, in_=src)
 
         def quant_w(s, t):
             nc.vector.quantize_mx(
                 out=wc[:, t, 4 * s : 4 * s + 4, :].rearrange("p g c -> p (g c)").bitcast(E4),
                 scales=ws[:, t, 4 * s : 4 * s + 4, :].rearrange("p g c -> p (g c)"),
-                in_=wu[(s, t)][:].rearrange("p g c j -> p (g c j)"),
+                in_=tiles[("wu", s, t)][:].rearrange("p g c j -> p (g c j)"),
             )
 
-        def passes_z(t, s, q):
+        def passes_z(q, t, s):
             a = psum.tile([P, 512], F32, name="az%d_%d_%d" % (t, s, q), tag="acc")
             for cm in range(4):
                 codes, plane, blk, win = zpos(s, q, cm)
@@ -155,18 +231,22 @@ def tile_groupwiselinearprojector_t_kernel(tc, x, Wg, bg, grad_out, out):
                     start=(cm == 0),
                     stop=(cm == 3),
                 )
-            acc[("z", t, s, q)] = a
+            tiles[("az", q, t, s)] = a
 
-        def evict_z(t, s, q, on_v):
-            dst = oz[(t, q)][:].rearrange("p (r4 rm c4 cm) -> p rm r4 c4 cm", r4=8, rm=4, c4=16, cm=4)[:, s]
-            src = acc[("z", t, s, q)][:].rearrange("p (cm r4 c4) -> p r4 c4 cm", cm=4, r4=8, c4=16)
-            if on_v:
+        def evict_z(eng, q, t, s):
+            k = ("oz", q, t)
+            if k not in tiles:
+                tiles[k] = work.tile([P, 2048], F32, name="oz%d_%d" % (t, q), tag="oz", bufs=3)
+            dst = tiles[k][:].rearrange("p (r4 rm c4 cm) -> p rm r4 c4 cm", r4=8, rm=4, c4=16, cm=4)[:, s]
+            src = tiles[("az", q, t, s)][:].rearrange("p (cm r4 c4) -> p r4 c4 cm", cm=4, r4=8, c4=16)
+            if eng == "V":
                 nc.vector.tensor_copy(out=dst, in_=src)
             else:
                 nc.scalar.copy(out=dst, in_=src)
-            if s == 3:
-                ov = out[0].rearrange("(t p) r c -> t p (r c)", p=P)
-                nc.sync.dma_start(out=ov[t][:, 2048 * q : 2048 * q + 2048], in_=oz[(t, q)][:])
+
+        def store_z(q, t):
+            ov = out[0].rearrange("(t p) r c -> t p (r c)", p=P)
+            nc.sync.dma_start(out=ov[t][:, 2048 * q : 2048 * q + 2048], in_=tiles[("oz", q, t)][:])
 
         def passes_j(t, s):
             for cm in range(4):
@@ -182,116 +262,105 @@ def tile_groupwiselinearprojector_t_kernel(tc, x, Wg, bg, grad_out, out):
                     start=True,
                     stop=True,
                 )
-                acc[("j", t, s, cm)] = a
+                tiles[("aj", t, s, cm)] = a
 
-        def evict_j(t, s):
-            ev[(t, s)] = work.tile([P, 4, 256], F32, name="ev%d_%d" % (t, s), tag="mid", bufs=6, align_bytes=64)
-            on_v = v_evicts_j(t, s)
-            for cm in on_v:
-                lo = 256 * (cm % 2)
-                nc.vector.tensor_copy(out=ev[(t, s)][:, cm, :], in_=acc[("j", t, s, cm)][:, lo : lo + 256])
-            for cm in range(4):
-                if cm not in on_v:
-                    lo = 256 * (cm % 2)
-                    nc.scalar.copy(out=ev[(t, s)][:, cm, :], in_=acc[("j", t, s, cm)][:, lo : lo + 256])
+        def evict_j(eng, t, s, cm):
+            k = ("ev", t, s)
+            if k not in tiles:
+                tiles[k] = work.tile([P, 4, 256], F32, name="ev%d_%d" % (t, s), tag="wv", bufs=3, align_bytes=64)
+            lo = 256 * (cm % 2)
+            if eng == "V":
+                nc.vector.tensor_copy(out=tiles[k][:, cm, :], in_=tiles[("aj", t, s, cm)][:, lo : lo + 256])
+            else:
+                nc.scalar.copy(out=tiles[k][:, cm, :], in_=tiles[("aj", t, s, cm)][:, lo : lo + 256])
 
         def interleave_j(t, s):
-            dst = osb[t][:].rearrange("p (r4 rm c4 cm) -> p rm r4 c4 cm", r4=16, rm=4, c4=16, cm=4)[:, s]
-            src = ev[(t, s)][:].rearrange("p cm (r4 c4) -> p r4 c4 cm", r4=16, c4=16)
+            k = ("osb", t)
+            if k not in tiles:
+                tiles[k] = work.tile([P, 4096], F32, name="osb%d" % t, tag="big", bufs=3)
+            dst = tiles[k][:].rearrange("p (r4 rm c4 cm) -> p rm r4 c4 cm", r4=16, rm=4, c4=16, cm=4)[:, s]
+            src = tiles[("ev", t, s)][:].rearrange("p cm (r4 c4) -> p r4 c4 cm", r4=16, c4=16)
             nc.vector.tensor_copy(out=dst, in_=src)
-            if s == 3:
-                ov = out[1].rearrange("(t p) r c -> t p (r c)", p=P)
-                nc.sync.dma_start(out=ov[t], in_=osb[t][:])
 
-        ezq = []
-        state = {"ez": 0, "z1": 0, "head": 0, "pend": [], "open": False, "w": None}
-        z1 = [(t, s, 1) for t in range(3) for s in range(4)]
+        def store_j(t):
+            ov = out[1].rearrange("(t p) r c -> t p (r c)", p=P)
+            nc.sync.dma_start(out=ov[t], in_=tiles[("osb", t)][:])
 
-        def flush():
-            for ci, rm in state["pend"]:
-                quant_g(ci, rm)
-            state["pend"] = []
-
-        def pop_ez(k):
-            for i in range(k):
-                if state["head"] < len(ezq):
-                    t, s, q = ezq[state["head"]]
-                    state["head"] = state["head"] + 1
-                    evict_z(t, s, q, state["ez"] % EZ_V_EVERY == EZ_V_EVERY - 1)
-                    state["ez"] = state["ez"] + 1
-
-        def issue(k):
-            for i in range(k):
-                if state["open"] and state["z1"] < len(z1):
-                    t, s, q = z1[state["z1"]]
-                    state["z1"] = state["z1"] + 1
-                    if s == 0:
-                        oz[(t, q)] = work.tile([P, 2048], F32, name="oz%d_%d" % (t, q), tag="oz", bufs=3)
-                    passes_z(t, s, q)
-                    ezq.append((t, s, q))
-
-        def finish_w():
-            if state["w"] is not None:
-                s_, t_ = state["w"]
-                quant_w(s_, t_)
-                passes_z(t_, s_, 0)
-                ezq.append((t_, s_, 0))
-                state["w"] = None
-
-        def do_g(ci, mid_work):
-            for rm in range(4):
-                regroup_g(ci, rm)
-            finish_w()
-            if mid_work:
-                pop_ez(PER_G)
-                issue(PER_G)
-            for rm in V_ROW_PHASES:
-                quant_g(ci, rm)
-            flush()
-            for rm in range(4):
-                if rm not in V_ROW_PHASES:
-                    state["pend"] = state["pend"] + [(ci, rm)]
-
-        for ci in range(2):
-            do_g(ci, False)
-        flush()
-        for t in range(3):
-            oz[(t, 0)] = work.tile([P, 2048], F32, name="oz%d_0" % t, tag="oz", bufs=3)
-        for s in range(4):
-            for t in range(3):
-                regroup_w(s, t)
-                if len(ezq) - state["head"] >= LAG:
-                    pop_ez(1)
-                finish_w()
-                state["w"] = (s, t)
-        for ci in range(2, 3):
-            do_g(ci, True)
-            pop_ez(PER_G)
-        flush()
-        state["open"] = True
-        issue(AHEAD)
-        for ci in range(3, 5):
-            do_g(ci, True)
-            pop_ez(PER_G)
-            issue(PER_G)
-        flush()
-        while state["head"] < len(ezq) or state["z1"] < len(z1):
-            pop_ez(1)
-            issue(1)
-
+        units = [(s, t) for s in range(4) for t in range(3)]
         stages = [(t, s) for t in range(3) for s in range(4)]
-        prev = None
-        for i, (t, s) in enumerate(stages):
-            if s == 0:
-                osb[t] = work.tile([P, 4096], F32, name="osb%d" % t, tag="big", bufs=3)
-            if i == 0:
-                passes_j(t, s)
-            evict_j(t, s)
-            if i + 1 < len(stages):
-                passes_j(stages[i + 1][0], stages[i + 1][1])
-            if prev is not None:
-                interleave_j(prev[0], prev[1])
-            prev = (t, s)
-            if s == 3:
-                interleave_j(t, s)
-                prev = None
+
+        def add(eng, tok):
+            k = tok[0]
+            if k == "zero":
+                op("V", ("zero",), [], zeros)
+            elif k == "rg":
+                c, rm, h = tok[1], tok[2], tok[3]
+                r0, n = PIECES[c][h]
+                op(eng, ("rg", c, rm, h), [("ld", c, h)], lambda: regroup_g(eng, c, rm, r0, n))
+            elif k == "qz":
+                q, rm = tok[1], tok[2]
+                deps = [("rg", q, rm, h) for h in range(len(PIECES[q]))]
+                if q == 1:
+                    deps = deps + [("pz", 0, t, rm) for t in range(3)]
+                op("V", ("qz", q, rm), deps, lambda: quant_z(q, rm))
+            elif k == "qj":
+                rm = tok[1]
+                op("V", ("qj", rm), [("rg", 2, rm, 0), ("rg", 3, rm, 0)], lambda: quant_j(rm))
+            elif k == "rw":
+                s, t, h = tok[1], tok[2], tok[3]
+                g0, g1 = WPIECES[s][h]
+                op(eng, ("rw", s, t, h), [("ldw", s, h)], lambda: regroup_w(eng, s, t, g0, g1))
+            elif k == "qw":
+                s, t = tok[1], tok[2]
+                op("V", ("qw", s, t), [("rw", s, t, h) for h in range(len(WPIECES[s]))], lambda: quant_w(s, t))
+            elif k == "ez":
+                q, t, s = tok[1], tok[2], tok[3]
+                op(eng, ("ez", q, t, s), [("pz", q, t, s)], lambda: evict_z(eng, q, t, s))
+            elif k == "ej":
+                t, s, cm = tok[1], tok[2], tok[3]
+                op(eng, ("ej", t, s, cm), [("pj", t, s)], lambda: evict_j(eng, t, s, cm))
+            elif k == "ij":
+                t, s = tok[1], tok[2]
+                op("V", ("ij", t, s), [("ej", t, s, cm) for cm in range(4)], lambda: interleave_j(t, s))
+            elif k == "pz":
+                q, t, s = tok[1], tok[2], tok[3]
+                op("PE", ("pz", q, t, s), [("qw", s, t), ("qz", q, s)], lambda: passes_z(q, t, s))
+            elif k == "pj":
+                t, s = tok[1], tok[2]
+                op("PE", ("pj", t, s), [("qw", s, t), ("qj", s)], lambda: passes_j(t, s))
+            elif k == "ld":
+                c, h = tok[1], tok[2]
+                r0, n = PIECES[c][h]
+                op("SP", ("ld", c, h), [], lambda: load_g(c, 256 * r0, 256 * (r0 + n)))
+            elif k == "ldw":
+                s, h = tok[1], tok[2]
+                g0, g1 = WPIECES[s][h]
+                op("SP", ("ldw", s, h), [], lambda: load_w(s, g0, g1))
+            elif k == "sz":
+                q, t = tok[1], tok[2]
+                op("SP", ("sz", q, t), [("ez", q, t, s) for s in range(4)], lambda: store_z(q, t))
+            elif k == "sj":
+                t = tok[1]
+                op("SP", ("sj", t), [("ij", t, s) for s in range(4)], lambda: store_j(t))
+
+        scripts = SCRIPTS(units, stages)
+        for eng in ("SP", "V", "S", "PE"):
+            for tok in scripts[eng]:
+                add(eng, tok)
+
+        done = set()
+        heads = {"SP": 0, "V": 0, "S": 0, "PE": 0}
+        left = sum(len(queues[e]) for e in queues)
+        while left > 0:
+            moved = 0
+            for e in ("SP", "V", "S", "PE"):
+                if heads[e] < len(queues[e]):
+                    k = queues[e][heads[e]]
+                    deps, fn = ops[k]
+                    if all(d in done for d in deps):
+                        fn()
+                        done.add(k)
+                        heads[e] = heads[e] + 1
+                        moved = moved + 1
+            assert moved > 0
+            left = left - moved

@@ -15,12 +15,23 @@ E5 = mybir.dt.float8_e5m2_x4
 P = 128
 UNIT = 640
 
-PIECES = {0: ((0, 1), (1, 1), (2, 2), (4, 2), (6, 2)), 1: ((0, 8),), 2: ((0, 8),), 3: ((0, 8),)}
+PIECES = {0: ((0, 4), (4, 4)), 1: ((0, 8),), 2: ((0, 8),), 3: ((0, 8),)}
 WPIECES = {0: ((0, 2), (2, 4)), 1: ((0, 4),), 2: ((0, 4),), 3: ((0, 4),)}
 A_V = (0, 1)
 V3 = "rgB0 rgB1 qzB0 qzB1 qzB2 qzB3 rgC0 rgD0 rgD1 qj0 rgC2 rgD2 qj1 rgD3 qj2 qj3"
-S3 = "rgB2 rgB3 ezA ezA ezA rgC1 ez ez ez ez rgC3 ez ez ez ez ez ez ez ez"
+S3 = "rgB2 rgB3 ezA ezA ezA rgC1 o o o o rgC3 o o o o o o o o"
 EJ_V = ((0, 3), (1, 3))
+EJ_FROM = 0
+LAST_STAGE = (2, 3)
+LAST_CUTS = 1
+ZV = ()
+TAIL = (("z", 0), ("z", 1), ("z", 2), ("j", 0), ("j", 1), ("j", 2))
+
+
+def cuts(t, s):
+    if (t, s) == LAST_STAGE:
+        return tuple((256 * i // LAST_CUTS, 256 * (i + 1) // LAST_CUTS) for i in range(LAST_CUTS))
+    return ((0, 256),)
 
 
 def SCRIPTS(units, stages):
@@ -32,18 +43,20 @@ def SCRIPTS(units, stages):
             SP.append(("ldw", s, h))
     for c in (1, 2, 3):
         SP.append(("ld", c, 0))
-    for q in range(2):
-        for t in range(3):
-            SP.append(("sz", q, t))
     for t in range(3):
-        SP.append(("sj", t))
+        SP.append(("sz", 0, t))
     for s, t in units:
         PE.append(("pz", 0, t, s))
-    zb = [(t, s) for t in range(3) for s in range(4)]
-    for t, s in zb:
-        PE.append(("pz", 1, t, s))
-    for t, s in stages:
-        PE.append(("pj", t, s))
+    tail = []
+    for kind, t in TAIL:
+        if kind == "z":
+            SP.append(("sz", 1, t))
+        else:
+            for x0, x1 in cuts(t, 3):
+                SP.append(("sj", t, x0, x1))
+        for s in range(4):
+            tail.append((kind, t, s))
+            PE.append(("pz", 1, t, s) if kind == "z" else ("pj", t, s))
     V.append(("zero",))
     for h in range(len(PIECES[0])):
         for rm in range(4):
@@ -68,9 +81,30 @@ def SCRIPTS(units, stages):
                 S.append(("ez", 0, t, s - 1))
     cn = {"B": 1, "C": 2, "D": 3}
     na = [9]
-    nb = [0]
+
+    def out_work(eng, isv, i):
+        if i < len(tail):
+            kind, t, s = tail[i]
+            if kind == "z":
+                if isv == (i in ZV):
+                    eng.append(("ez", 1, t, s))
+            else:
+                for x0, x1 in cuts(t, s):
+                    for cm in range(4):
+                        if isv == ((i % 2, cm) in EJ_V and i >= EJ_FROM):
+                            eng.append(("ej", t, s, cm, x0, x1))
+                    if isv and len(cuts(t, s)) > 1:
+                        eng.append(("ij", t, s, x0, x1))
+        if isv and 1 <= i and tail[i - 1][0] == "j" and len(cuts(tail[i - 1][1], tail[i - 1][2])) == 1:
+            eng.append(("ij", tail[i - 1][1], tail[i - 1][2], 0, 256))
+
     for eng, txt in ((V, V3), (S, S3)):
+        n = 0
         for w in txt.split():
+            if w == "o":
+                out_work(eng, eng is V, n)
+                n = n + 1
+                continue
             if w.startswith("rg"):
                 eng.append(("rg", cn[w[2]], int(w[3]), 0))
             elif w.startswith("qz"):
@@ -81,16 +115,9 @@ def SCRIPTS(units, stages):
                 s_, t_ = units[na[0]]
                 na[0] = na[0] + 1
                 eng.append(("ez", 0, t_, s_))
-            elif w == "ez":
-                t_, s_ = zb[nb[0]]
-                nb[0] = nb[0] + 1
-                eng.append(("ez", 1, t_, s_))
-    for i, (t, s) in enumerate(stages):
-        for cm in range(4):
-            (V if (i % 2, cm) in EJ_V else S).append(("ej", t, s, cm))
-        if i >= 1:
-            V.append(("ij",) + stages[i - 1])
-    V.append(("ij", 2, 3))
+        while n <= len(tail):
+            out_work(eng, eng is V, n)
+            n = n + 1
     return {"SP": SP, "V": V, "S": S, "PE": PE}
 
 
@@ -145,15 +172,12 @@ def tile_groupwiselinearprojector_t_kernel(tc, x, Wg, bg, grad_out, out):
 
         wv = Wg.rearrange("g (p j) c -> p g (j c)", j=4)
 
-        def raw_tile(c):
-            if ("raw", c) not in tiles:
-                tiles[("raw", c)] = work.tile([P, 4, 2048], BF16, name="rawg%d" % c, tag="big", bufs=3)
-            return tiles[("raw", c)]
-
-        def load_g(c, lo, hi):
+        def load_g(c, h):
+            r0, n = PIECES[c][h]
+            tiles[("raw", c, h)] = work.tile([P, 4, 256 * n], BF16, name="rawg%d_%d" % (c, h), tag="big", bufs=3)
             gv = grad_out[c // 2].rearrange("(p j) r c -> p j (r c)", j=4)
-            o = 2048 * (c % 2)
-            nc.sync.dma_start(out=raw_tile(c)[:, :, lo:hi], in_=gv[:, :, o + lo : o + hi])
+            o = 2048 * (c % 2) + 256 * r0
+            nc.sync.dma_start(out=tiles[("raw", c, h)][:], in_=gv[:, :, o : o + 256 * n])
 
         def load_w(s, g0, g1):
             if ("raww", s) not in tiles:
@@ -169,8 +193,9 @@ def tile_groupwiselinearprojector_t_kernel(tc, x, Wg, bg, grad_out, out):
                     tiles[k] = work.tile([P, 4, 256, 4], BF16, name="gj_%d" % rm, tag="raww", bufs=4, align_bytes=64)
             return tiles[k]
 
-        def regroup_g(eng, c, rm, r0, n):
-            src = raw_tile(c)[:].rearrange("p t (r4 rm c4 cm) -> p rm r4 c4 t cm", r4=8, rm=4, c4=16, cm=4)[:, rm, r0 : r0 + n]
+        def regroup_g(eng, c, rm, h):
+            r0, n = PIECES[c][h]
+            src = tiles[("raw", c, h)][:].rearrange("p t (r4 rm c4 cm) -> p rm r4 c4 t cm", r4=n, rm=4, c4=16, cm=4)[:, rm]
             o = 0 if c < 3 else 8
             dst = gu_tile(c, rm)[:].rearrange("p cm (r4 c4) t -> p r4 c4 t cm", c4=16)[:, o + r0 : o + r0 + n]
             if eng == "V":
@@ -264,27 +289,27 @@ def tile_groupwiselinearprojector_t_kernel(tc, x, Wg, bg, grad_out, out):
                 )
                 tiles[("aj", t, s, cm)] = a
 
-        def evict_j(eng, t, s, cm):
+        def evict_j(eng, t, s, cm, x0, x1):
             k = ("ev", t, s)
             if k not in tiles:
                 tiles[k] = work.tile([P, 4, 256], F32, name="ev%d_%d" % (t, s), tag="wv", bufs=3, align_bytes=64)
             lo = 256 * (cm % 2)
             if eng == "V":
-                nc.vector.tensor_copy(out=tiles[k][:, cm, :], in_=tiles[("aj", t, s, cm)][:, lo : lo + 256])
+                nc.vector.tensor_copy(out=tiles[k][:, cm, x0:x1], in_=tiles[("aj", t, s, cm)][:, lo + x0 : lo + x1])
             else:
-                nc.scalar.copy(out=tiles[k][:, cm, :], in_=tiles[("aj", t, s, cm)][:, lo : lo + 256])
+                nc.scalar.copy(out=tiles[k][:, cm, x0:x1], in_=tiles[("aj", t, s, cm)][:, lo + x0 : lo + x1])
 
-        def interleave_j(t, s):
+        def interleave_j(t, s, x0, x1):
             k = ("osb", t)
             if k not in tiles:
                 tiles[k] = work.tile([P, 4096], F32, name="osb%d" % t, tag="big", bufs=3)
-            dst = tiles[k][:].rearrange("p (r4 rm c4 cm) -> p rm r4 c4 cm", r4=16, rm=4, c4=16, cm=4)[:, s]
-            src = tiles[("ev", t, s)][:].rearrange("p cm (r4 c4) -> p r4 c4 cm", r4=16, c4=16)
+            dst = tiles[k][:].rearrange("p (r4 rm c4 cm) -> p rm r4 c4 cm", r4=16, rm=4, c4=16, cm=4)[:, s, x0 // 16 : x1 // 16]
+            src = tiles[("ev", t, s)][:].rearrange("p cm (r4 c4) -> p r4 c4 cm", r4=16, c4=16)[:, x0 // 16 : x1 // 16]
             nc.vector.tensor_copy(out=dst, in_=src)
 
-        def store_j(t):
+        def store_j(t, x0, x1):
             ov = out[1].rearrange("(t p) r c -> t p (r c)", p=P)
-            nc.sync.dma_start(out=ov[t], in_=tiles[("osb", t)][:])
+            nc.sync.dma_start(out=ov[t][:, 16 * x0 : 16 * x1], in_=tiles[("osb", t)][:, 16 * x0 : 16 * x1])
 
         units = [(s, t) for s in range(4) for t in range(3)]
         stages = [(t, s) for t in range(3) for s in range(4)]
@@ -295,8 +320,7 @@ def tile_groupwiselinearprojector_t_kernel(tc, x, Wg, bg, grad_out, out):
                 op("V", ("zero",), [], zeros)
             elif k == "rg":
                 c, rm, h = tok[1], tok[2], tok[3]
-                r0, n = PIECES[c][h]
-                op(eng, ("rg", c, rm, h), [("ld", c, h)], lambda: regroup_g(eng, c, rm, r0, n))
+                op(eng, ("rg", c, rm, h), [("ld", c, h)], lambda: regroup_g(eng, c, rm, h))
             elif k == "qz":
                 q, rm = tok[1], tok[2]
                 deps = [("rg", q, rm, h) for h in range(len(PIECES[q]))]
@@ -317,11 +341,11 @@ def tile_groupwiselinearprojector_t_kernel(tc, x, Wg, bg, grad_out, out):
                 q, t, s = tok[1], tok[2], tok[3]
                 op(eng, ("ez", q, t, s), [("pz", q, t, s)], lambda: evict_z(eng, q, t, s))
             elif k == "ej":
-                t, s, cm = tok[1], tok[2], tok[3]
-                op(eng, ("ej", t, s, cm), [("pj", t, s)], lambda: evict_j(eng, t, s, cm))
+                t, s, cm, x0, x1 = tok[1], tok[2], tok[3], tok[4], tok[5]
+                op(eng, ("ej", t, s, cm, x0), [("pj", t, s)], lambda: evict_j(eng, t, s, cm, x0, x1))
             elif k == "ij":
-                t, s = tok[1], tok[2]
-                op("V", ("ij", t, s), [("ej", t, s, cm) for cm in range(4)], lambda: interleave_j(t, s))
+                t, s, x0, x1 = tok[1], tok[2], tok[3], tok[4]
+                op("V", ("ij", t, s, x0), [("ej", t, s, cm, x0) for cm in range(4)], lambda: interleave_j(t, s, x0, x1))
             elif k == "pz":
                 q, t, s = tok[1], tok[2], tok[3]
                 op("PE", ("pz", q, t, s), [("qw", s, t), ("qz", q, s)], lambda: passes_z(q, t, s))
@@ -330,8 +354,7 @@ def tile_groupwiselinearprojector_t_kernel(tc, x, Wg, bg, grad_out, out):
                 op("PE", ("pj", t, s), [("qw", s, t), ("qj", s)], lambda: passes_j(t, s))
             elif k == "ld":
                 c, h = tok[1], tok[2]
-                r0, n = PIECES[c][h]
-                op("SP", ("ld", c, h), [], lambda: load_g(c, 256 * r0, 256 * (r0 + n)))
+                op("SP", ("ld", c, h), [], lambda: load_g(c, h))
             elif k == "ldw":
                 s, h = tok[1], tok[2]
                 g0, g1 = WPIECES[s][h]
@@ -340,8 +363,9 @@ def tile_groupwiselinearprojector_t_kernel(tc, x, Wg, bg, grad_out, out):
                 q, t = tok[1], tok[2]
                 op("SP", ("sz", q, t), [("ez", q, t, s) for s in range(4)], lambda: store_z(q, t))
             elif k == "sj":
-                t = tok[1]
-                op("SP", ("sj", t), [("ij", t, s) for s in range(4)], lambda: store_j(t))
+                t, x0, x1 = tok[1], tok[2], tok[3]
+                deps = [("ij", t, s, 0) for s in range(3)] + [("ij", t, 3, x0)]
+                op("SP", ("sj", t, x0), deps, lambda: store_j(t, x0, x1))
 
         scripts = SCRIPTS(units, stages)
         for eng in ("SP", "V", "S", "PE"):

@@ -225,7 +225,7 @@ def tile_groupwiselinearprojector_t_kernel(tc, x, Wg, bg, grad_out, out):
                 if eng == "V":
                     tiles[k] = work.tile([P, 4, 128, 4], BF16, name="wu%d_%d" % (s, t), tag="wv", bufs=3, align_bytes=64)
                 else:
-                    tiles[k] = work.tile([P, 4, 128, 4], BF16, name="wu%d_%d" % (s, t), tag="wq", bufs=2, align_bytes=64)
+                    tiles[k] = work.tile([P, 4, 128, 4], BF16, name="wu%d_%d" % (s, t), tag="gu", bufs=4, align_bytes=64)
             src = tiles[("raww", s)][:].rearrange("p g (j c) -> p g j c", j=4)[
                 :, g0:g1, :, 128 * t : 128 * t + 128
             ].rearrange("p g j (c i) -> p g c j i", i=4)
@@ -261,7 +261,7 @@ def tile_groupwiselinearprojector_t_kernel(tc, x, Wg, bg, grad_out, out):
         def evict_z(eng, q, t, s):
             k = ("oz", q, t)
             if k not in tiles:
-                tiles[k] = work.tile([P, 2048], F32, name="oz%d_%d" % (t, q), tag="oz", bufs=3)
+                tiles[k] = work.tile([P, 2048], F32, name="oz%d_%d" % (t, q), tag="oz", bufs=4)
             dst = tiles[k][:].rearrange("p (r4 rm c4 cm) -> p rm r4 c4 cm", r4=8, rm=4, c4=16, cm=4)[:, s]
             src = tiles[("az", q, t, s)][:].rearrange("p (cm r4 c4) -> p r4 c4 cm", cm=4, r4=8, c4=16)
             if eng == "V":

@@ -17,7 +17,10 @@ UNIT = 640
 
 PIECES = {0: ((0, 4), (4, 4)), 1: ((0, 8),), 2: ((0, 8),), 3: ((0, 8),)}
 WPIECES = {0: ((0, 2), (2, 4)), 1: ((0, 4),), 2: ((0, 4),), 3: ((0, 4),)}
+HEAD = "A"
 A_V = (0, 1)
+A_S = ((1, 1),)
+W1_CUT = (16, 28, 28, 28)
 V3 = "rgB0 rgB1 qzB0 qzB1 qzB2 qzB3 rgC0 rgD0 rgD1 qj0 rgC2 rgD2 qj1 rgD3 qj2 qj3"
 S3 = "rgB2 rgB3 ezA ezA ezA rgC1 o o o o rgC3 o o o o o o o o"
 EJ_V = ((0, 3), (1, 3))
@@ -25,7 +28,7 @@ EJ_FROM = 0
 LAST_STAGE = (2, 3)
 LAST_CUTS = 1
 ZV = ()
-TAIL = (("z", 0), ("z", 1), ("z", 2), ("j", 0), ("j", 1), ("j", 2))
+TAIL = "z00 z01 z02 z03 z10 z11 z12 z13 z20 z21 z22 z23 j00 j01 j02 j03 j10 j11 j12 j13 j20 j21 j22 j23"
 
 
 def cuts(t, s):
@@ -36,11 +39,15 @@ def cuts(t, s):
 
 def SCRIPTS(units, stages):
     V, S, PE, SP = [], [], [], []
+    if HEAD == "W":
+        for h in range(len(WPIECES[0])):
+            SP.append(("ldw", 0, h))
     for h in range(len(PIECES[0])):
         SP.append(("ld", 0, h))
     for s in range(4):
         for h in range(len(WPIECES[s])):
-            SP.append(("ldw", s, h))
+            if not (HEAD == "W" and s == 0):
+                SP.append(("ldw", s, h))
     for c in (1, 2, 3):
         SP.append(("ld", c, 0))
     for t in range(3):
@@ -48,34 +55,50 @@ def SCRIPTS(units, stages):
     for s, t in units:
         PE.append(("pz", 0, t, s))
     tail = []
-    for kind, t in TAIL:
-        if kind == "z":
-            SP.append(("sz", 1, t))
-        else:
-            for x0, x1 in cuts(t, 3):
-                SP.append(("sj", t, x0, x1))
-        for s in range(4):
-            tail.append((kind, t, s))
-            PE.append(("pz", 1, t, s) if kind == "z" else ("pj", t, s))
+    for w in TAIL.split():
+        kind, t, s = w[0], int(w[1]), int(w[2])
+        tail.append((kind, t, s))
+        PE.append(("pz", 1, t, s) if kind == "z" else ("pj", t, s))
+        if s == 3:
+            if kind == "z":
+                SP.append(("sz", 1, t))
+            else:
+                for x0, x1 in cuts(t, 3):
+                    SP.append(("sj", t, x0, x1))
     V.append(("zero",))
-    for h in range(len(PIECES[0])):
-        for rm in range(4):
-            (V if rm in A_V else S).append(("rg", 0, rm, h))
-    V.append(("qz", 0, 0))
-    V.append(("qz", 0, 1))
+
+    def chunk_a():
+        for h in range(len(PIECES[0])):
+            for rm in range(4):
+                (V if (rm in A_V and (h, rm) not in A_S) else S).append(("rg", 0, rm, h))
+        V.append(("qz", 0, 0))
+        V.append(("qz", 0, 1))
+        if HEAD == "W":
+            V.append(("qz", 0, 2))
+            V.append(("qz", 0, 3))
+
+    if HEAD == "A":
+        chunk_a()
     for s in range(4):
+        cut = W1_CUT[s]
         for h in range(len(WPIECES[s])):
-            V.append(("rw", s, 0, h))
-            if s == 0 and h == 0:
+            V.append(("rw", s, 0, h, 0, 32))
+            if s == 0 and h == 0 and HEAD == "A":
                 V.append(("qz", 0, 2))
         for h in range(len(WPIECES[s])):
-            V.append(("rw", s, 1, h))
-            S.append(("rw", s, 2, h))
+            if cut > 0:
+                V.append(("rw", s, 1, h, 0, cut))
+            if cut < 32:
+                S.append(("rw", s, 1, h, cut, 32))
+        for h in range(len(WPIECES[s])):
+            S.append(("rw", s, 2, h, 0, 32))
         V.append(("qw", s, 0))
-        if s == 0:
+        if s == 0 and HEAD == "A":
             V.append(("qz", 0, 3))
         V.append(("qw", s, 1))
         V.append(("qw", s, 2))
+        if s == 0 and HEAD == "W":
+            chunk_a()
         if s >= 1:
             for t in range(3):
                 S.append(("ez", 0, t, s - 1))
@@ -219,17 +242,17 @@ def tile_groupwiselinearprojector_t_kernel(tc, x, Wg, bg, grad_out, out):
                 in_=gu_tile(2, rm)[:].rearrange("p g x t -> p (g x t)"),
             )
 
-        def regroup_w(eng, s, t, g0, g1):
+        def regroup_w(eng, s, t, g0, g1, c0, c1):
             k = ("wu", s, t)
             if k not in tiles:
-                if eng == "V":
+                if t < 2:
                     tiles[k] = work.tile([P, 4, 128, 4], BF16, name="wu%d_%d" % (s, t), tag="wv", bufs=3, align_bytes=64)
                 else:
                     tiles[k] = work.tile([P, 4, 128, 4], BF16, name="wu%d_%d" % (s, t), tag="gu", bufs=4, align_bytes=64)
             src = tiles[("raww", s)][:].rearrange("p g (j c) -> p g j c", j=4)[
-                :, g0:g1, :, 128 * t : 128 * t + 128
+                :, g0:g1, :, 128 * t + 4 * c0 : 128 * t + 4 * c1
             ].rearrange("p g j (c i) -> p g c j i", i=4)
-            dst = tiles[k][:].rearrange("p g (c i) j -> p g c j i", i=4)[:, g0:g1]
+            dst = tiles[k][:].rearrange("p g (c i) j -> p g c j i", i=4)[:, g0:g1, c0:c1]
             if eng == "V":
                 nc.vector.tensor_copy(out=dst, in_=src)
             else:
@@ -331,12 +354,15 @@ def tile_groupwiselinearprojector_t_kernel(tc, x, Wg, bg, grad_out, out):
                 rm = tok[1]
                 op("V", ("qj", rm), [("rg", 2, rm, 0), ("rg", 3, rm, 0)], lambda: quant_j(rm))
             elif k == "rw":
-                s, t, h = tok[1], tok[2], tok[3]
+                s, t, h, c0, c1 = tok[1], tok[2], tok[3], tok[4], tok[5]
                 g0, g1 = WPIECES[s][h]
-                op(eng, ("rw", s, t, h), [("ldw", s, h)], lambda: regroup_w(eng, s, t, g0, g1))
+                op(eng, ("rw", s, t, h, c0), [("ldw", s, h)], lambda: regroup_w(eng, s, t, g0, g1, c0, c1))
             elif k == "qw":
                 s, t = tok[1], tok[2]
-                op("V", ("qw", s, t), [("rw", s, t, h) for h in range(len(WPIECES[s]))], lambda: quant_w(s, t))
+                deps = [("rw", s, t, h, 0) for h in range(len(WPIECES[s]))]
+                if t == 1 and 0 < W1_CUT[s] < 32:
+                    deps = deps + [("rw", s, t, h, W1_CUT[s]) for h in range(len(WPIECES[s]))]
+                op("V", ("qw", s, t), deps, lambda: quant_w(s, t))
             elif k == "ez":
                 q, t, s = tok[1], tok[2], tok[3]
                 op(eng, ("ez", q, t, s), [("pz", q, t, s)], lambda: evict_z(eng, q, t, s))

@@ -23,7 +23,7 @@ A_S = ((1, 1),)
 W1_CUT = (16, 28, 28, 28)
 V3 = "rgB0 rgB1 qzB0 qzB1 qzB2 qzB3 rgC0 rgD0 rgD1 qj0 rgC2 rgD2 qj1 rgD3 qj2 qj3"
 S3 = "rgB2 rgB3 ezA ezA ezA rgC1 o o o o rgC3 o o o o o o o o"
-EJ_V = ((0, 3), (1, 3))
+EJ_V = ()
 EJ_FROM = 0
 LAST_STAGE = (2, 3)
 LAST_CUTS = 1

@@ -284,7 +284,10 @@ def tile_groupwiselinearprojector_t_kernel(tc, x, Wg, bg, grad_out, out):
         def evict_z(eng, q, t, s):
             k = ("oz", q, t)
             if k not in tiles:
-                tiles[k] = work.tile([P, 2048], F32, name="oz%d_%d" % (t, q), tag="oz", bufs=4)
+                if (q, t) == (1, 1):
+                    tiles[k] = work.tile([P, 2048], F32, name="oz%d_%d" % (t, q), tag="big", bufs=3)
+                else:
+                    tiles[k] = work.tile([P, 2048], F32, name="oz%d_%d" % (t, q), tag="oz", bufs=4)
             dst = tiles[k][:].rearrange("p (r4 rm c4 cm) -> p rm r4 c4 cm", r4=8, rm=4, c4=16, cm=4)[:, s]
             src = tiles[("az", q, t, s)][:].rearrange("p (cm r4 c4) -> p r4 c4 cm", cm=4, r4=8, c4=16)
             if eng == "V":

@@ -329,8 +329,8 @@ def tile_groupwiselinearprojector_t_kernel(tc, x, Wg, bg, grad_out, out):
             k = ("osb", t)
             if k not in tiles:
                 tiles[k] = work.tile([P, 4096], F32, name="osb%d" % t, tag="big", bufs=3)
-            dst = tiles[k][:].rearrange("p (r4 rm c4 cm) -> p rm r4 c4 cm", r4=16, rm=4, c4=16, cm=4)[:, s, x0 // 16 : x1 // 16]
-            src = tiles[("ev", t, s)][:].rearrange("p cm (r4 c4) -> p r4 c4 cm", r4=16, c4=16)[:, x0 // 16 : x1 // 16]
+            dst = tiles[k][:].rearrange("p (r4 rm c i cm) -> p rm r4 c cm i", r4=16, rm=4, c=4, i=4, cm=4)[:, s, x0 // 16 : x1 // 16]
+            src = tiles[("ev", t, s)][:].rearrange("p cm (r4 c i) -> p r4 c cm i", r4=16, c=4, i=4)[:, x0 // 16 : x1 // 16]
             nc.vector.tensor_copy(out=dst, in_=src)
 
         def store_j(t, x0, x1):

from contextlib import ExitStack

import concourse.mybir as mybir

FLOPS = 2 * 16 * 512 * 512 * 384
BYTES = 2 * 512 * 4096 * 2 + 16 * 512 * 384 * 2 + 2 * 384 * 4096 * 4

BF16 = mybir.dt.bfloat16
F32 = mybir.dt.float32
I32 = mybir.dt.int32
U32 = mybir.dt.uint32
U8 = mybir.dt.uint8
E4 = mybir.dt.float8_e4m3fn_x4
E5 = mybir.dt.float8_e5m2_x4
P = 128
UNIT = 640

PIECES = {0: ((0, 4), (4, 4)), 1: ((0, 8),), 2: ((0, 8),), 3: ((0, 8),)}
WPIECES = {0: ((0, 2), (2, 4)), 1: ((0, 4),), 2: ((0, 4),), 3: ((0, 4),)}
HEAD = "A"
A_V = (0, 1)
A_S = ((1, 1),)
W1_CUT = (16, 28, 28, 28)
V3 = "rgB0 rgB1 qzB0 qzB1 qzB2 qzB3 rgC0 rgD0 rgD1 qj0 rgC2 rgD2 qj1 rgD3 qj2 qj3"
S3 = "rgB2 rgB3 ezA ezA ezA rgC1 o o o o rgC3 o o o o o o o o"
EJ_V = ()
EJ_FROM = 0
LAST_STAGE = (2, 3)
LAST_CUTS = 1
ZV = ()
TAIL = "z00 z01 z02 z03 z10 z11 z12 z13 z20 z21 z22 z23 j00 j01 j02 j03 j10 j11 j12 j13 j20 j21 j22 j23"


def cuts(t, s):
    if (t, s) == LAST_STAGE:
        return tuple((256 * i // LAST_CUTS, 256 * (i + 1) // LAST_CUTS) for i in range(LAST_CUTS))
    return ((0, 256),)


def SCRIPTS(units, stages):
    V, S, PE, SP = [], [], [], []
    if HEAD == "W":
        for h in range(len(WPIECES[0])):
            SP.append(("ldw", 0, h))
    for h in range(len(PIECES[0])):
        SP.append(("ld", 0, h))
    for s in range(4):
        for h in range(len(WPIECES[s])):
            if not (HEAD == "W" and s == 0):
                SP.append(("ldw", s, h))
    for c in (1, 2, 3):
        SP.append(("ld", c, 0))
    for t in range(3):
        SP.append(("sz", 0, t))
    for s, t in units:
        PE.append(("pz", 0, t, s))
    tail = []
    for w in TAIL.split():
        kind, t, s = w[0], int(w[1]), int(w[2])
        tail.append((kind, t, s))
        PE.append(("pz", 1, t, s) if kind == "z" else ("pj", t, s))
        if s == 3:
            if kind == "z":
                SP.append(("sz", 1, t))
            else:
                for x0, x1 in cuts(t, 3):
                    SP.append(("sj", t, x0, x1))
    V.append(("zero",))

    def chunk_a():
        for h in range(len(PIECES[0])):
            for rm in range(4):
                (V if (rm in A_V and (h, rm) not in A_S) else S).append(("rg", 0, rm, h))
        V.append(("qz", 0, 0))
        V.append(("qz", 0, 1))
        if HEAD == "W":
            V.append(("qz", 0, 2))
            V.append(("qz", 0, 3))

    if HEAD == "A":
        chunk_a()
    for s in range(4):
        cut = W1_CUT[s]
        for h in range(len(WPIECES[s])):
            V.append(("rw", s, 0, h, 0, 32))
            if s == 0 and h == 0 and HEAD == "A":
                V.append(("qz", 0, 2))
        for h in range(len(WPIECES[s])):
            if cut > 0:
                V.append(("rw", s, 1, h, 0, cut))
            if cut < 32:
                S.append(("rw", s, 1, h, cut, 32))
        for h in range(len(WPIECES[s])):
            S.append(("rw", s, 2, h, 0, 32))
        V.append(("qw", s, 0))
        if s == 0 and HEAD == "A":
            V.append(("qz", 0, 3))
        V.append(("qw", s, 1))
        V.append(("qw", s, 2))
        if s == 0 and HEAD == "W":
            chunk_a()
        if s >= 1:
            for t in range(3):
                S.append(("ez", 0, t, s - 1))
    cn = {"B": 1, "C": 2, "D": 3}
    na = [9]

    def out_work(eng, isv, i):
        if i < len(tail):
            kind, t, s = tail[i]
            if kind == "z":
                if isv == (i in ZV):
                    eng.append(("ez", 1, t, s))
            else:
                for x0, x1 in cuts(t, s):
                    for cm in range(4):
                        if isv == ((i % 2, cm) in EJ_V and i >= EJ_FROM):
                            eng.append(("ej", t, s, cm, x0, x1))
                    if isv and len(cuts(t, s)) > 1:
                        eng.append(("ij", t, s, x0, x1))
        if isv and 1 <= i and tail[i - 1][0] == "j" and len(cuts(tail[i - 1][1], tail[i - 1][2])) == 1:
            eng.append(("ij", tail[i - 1][1], tail[i - 1][2], 0, 256))

    for eng, txt in ((V, V3), (S, S3)):
        n = 0
        for w in txt.split():
            if w == "o":
                out_work(eng, eng is V, n)
                n = n + 1
                continue
            if w.startswith("rg"):
                eng.append(("rg", cn[w[2]], int(w[3]), 0))
            elif w.startswith("qz"):
                eng.append(("qz", 1, int(w[3])))
            elif w.startswith("qj"):
                eng.append(("qj", int(w[2])))
            elif w == "ezA":
                s_, t_ = units[na[0]]
                na[0] = na[0] + 1
                eng.append(("ez", 0, t_, s_))
        while n <= len(tail):
            out_work(eng, eng is V, n)
            n = n + 1
    return {"SP": SP, "V": V, "S": S, "PE": PE}


def tile_groupwiselinearprojector_t_kernel(tc, x, Wg, bg, grad_out, out):
    nc = tc.nc
    with ExitStack() as ctx:
        ctx.enter_context(tc.manual_schedule())
        keep = ctx.enter_context(tc.tile_pool(name="keep", bufs=1))
        work = ctx.enter_context(tc.tile_pool(name="work", bufs=1))
        psum = ctx.enter_context(tc.psum_pool(name="psum", bufs=8))

        g_a = keep.tile([P, 4 * UNIT], U32, name="g_a", align_bytes=64)
        g_as = keep.tile([P, 4 * UNIT], U8, name="g_as", align_bytes=64)
        g_b = keep.tile([P, 4 * UNIT + 128], U32, name="g_b", align_bytes=64)
        g_bs = keep.tile([P, 4 * UNIT + 128], U8, name="g_bs", align_bytes=64)
        g1c = keep.tile([P, 16, 256], U32, name="g1c", align_bytes=64)
        g1s = keep.tile([P, 16, 256], U8, name="g1s", align_bytes=64)
        wc = keep.tile([P, 3, 16, 128], U32, name="wc", align_bytes=64)
        ws = keep.tile([P, 3, 16, 128], U8, name="ws", align_bytes=64)

        tiles = {}
        queues = {"V": [], "S": [], "PE": [], "SP": []}
        ops = {}

        def op(eng, key, deps, fn):
            queues[eng].append(key)
            ops[key] = (deps, fn)

        def zpos(rm, q, cm):
            base = UNIT * rm
            if cm == 0:
                return g_a, g_as, base, base
            if cm == 3:
                return g_a, g_as, base + 512, base + 128
            if cm == 1:
                return g_b, g_bs, base + 128, base
            return g_b, g_bs, base + 512, base + 256

        def zero(tile_, words_per_unit, lo, hi):
            v = tile_[:].bitcast(I32)[:, 0 : 4 * words_per_unit].rearrange("p (u w) -> p u w", w=words_per_unit)
            nc.vector.memset(v[:, :, lo:hi], 0)

        def zeros():
            zero(g_a, UNIT, 128, 512)
            zero(g_b, UNIT, 0, 128)
            zero(g_b, UNIT, 256, 512)
            nc.vector.memset(g_b[:].bitcast(I32)[:, 4 * UNIT : 4 * UNIT + 128], 0)
            zero(g_as, UNIT // 4, 32, 128)
            zero(g_bs, UNIT // 4, 0, 32)
            zero(g_bs, UNIT // 4, 64, 128)
            nc.vector.memset(g_bs[:].bitcast(I32)[:, UNIT : UNIT + 32], 0)

        wv = Wg.rearrange("g (p j) c -> p g (j c)", j=4)

        def load_g(c, h):
            r0, n = PIECES[c][h]
            tiles[("raw", c, h)] = work.tile([P, 4, 256 * n], BF16, name="rawg%d_%d" % (c, h), tag="big", bufs=3)
            gv = grad_out[c // 2].rearrange("(p j) r c -> p j (r c)", j=4)
            o = 2048 * (c % 2) + 256 * r0
            nc.sync.dma_start(out=tiles[("raw", c, h)][:], in_=gv[:, :, o : o + 256 * n])

        def load_w(s, g0, g1):
            if ("raww", s) not in tiles:
                tiles[("raww", s)] = work.tile([P, 4, 1536], BF16, name="raww%d" % s, tag="raww", bufs=4, align_bytes=64)
            nc.sync.dma_start(out=tiles[("raww", s)][:, g0:g1, :], in_=wv[:, 4 * s + g0 : 4 * s + g1, :])

        def gu_tile(c, rm):
            k = ("gu", c, rm) if c < 2 else ("gu", 2, rm)
            if k not in tiles:
                if c < 2:
                    tiles[k] = work.tile([P, 4, 128, 4], BF16, name="gu%d_%d" % (c, rm), tag="gu", bufs=4, align_bytes=64)
                else:
                    tiles[k] = work.tile([P, 4, 256, 4], BF16, name="gj_%d" % rm, tag="raww", bufs=4, align_bytes=64)
            return tiles[k]

        def regroup_g(eng, c, rm, h):
            r0, n = PIECES[c][h]
            src = tiles[("raw", c, h)][:].rearrange("p t (r4 rm c4 cm) -> p rm r4 c4 t cm", r4=n, rm=4, c4=16, cm=4)[:, rm]
            o = 0 if c < 3 else 8
            dst = gu_tile(c, rm)[:].rearrange("p cm (r4 c4) t -> p r4 c4 t cm", c4=16)[:, o + r0 : o + r0 + n]
            if eng == "V":
                nc.vector.tensor_copy(out=dst, in_=src)
            else:
                nc.scalar.copy(out=dst, in_=src)

        def quant_z(q, rm):
            for cm in range(4):
                codes, plane, blk, win = zpos(rm, q, cm)
                nc.vector.quantize_mx(
                    out=codes[:, blk : blk + 128].bitcast(E5),
                    scales=plane[:, blk : blk + 128],
                    in_=gu_tile(q, rm)[:, cm].rearrange("p x t -> p (x t)"),
                )

        def quant_j(rm):
            nc.vector.quantize_mx(
                out=g1c[:, 4 * rm : 4 * rm + 4, :].rearrange("p g x -> p (g x)").bitcast(E5),
                scales=g1s[:, 4 * rm : 4 * rm + 4, :].rearrange("p g x -> p (g x)"),
                in_=gu_tile(2, rm)[:].rearrange("p g x t -> p (g x t)"),
            )

        def regroup_w(eng, s, t, g0, g1, c0, c1):
            k = ("wu", s, t)
            if k not in tiles:
                if t < 2:
                    tiles[k] = work.tile([P, 4, 128, 4], BF16, name="wu%d_%d" % (s, t), tag="wv", bufs=3, align_bytes=64)
                else:
                    tiles[k] = work.tile([P, 4, 128, 4], BF16, name="wu%d_%d" % (s, t), tag="gu", bufs=4, align_bytes=64)
            src = tiles[("raww", s)][:].rearrange("p g (j c) -> p g j c", j=4)[
                :, g0:g1, :, 128 * t + 4 * c0 : 128 * t + 4 * c1
            ].rearrange("p g j (c i) -> p g c j i", i=4)
            dst = tiles[k][:].rearrange("p g (c i) j -> p g c j i", i=4)[:, g0:g1, c0:c1]
            if eng == "V":
                nc.vector.tensor_copy(out=dst, in_=src)
            else:
                nc.scalar.copy(out=dst, in_=src)

        def quant_w(s, t):
            nc.vector.quantize_mx(
                out=wc[:, t, 4 * s : 4 * s + 4, :].rearrange("p g c -> p (g c)").bitcast(E4),
                scales=ws[:, t, 4 * s : 4 * s + 4, :].rearrange("p g c -> p (g c)"),
                in_=tiles[("wu", s, t)][:].rearrange("p g c j -> p (g c j)"),
            )

        def passes_z(q, t, s):
            a = psum.tile([P, 512], F32, name="az%d_%d_%d" % (t, s, q), tag="acc")
            for cm in range(4):
                codes, plane, blk, win = zpos(s, q, cm)
                g = 4 * s + cm
                nc.tensor.matmul_mx(
                    out=a[:],
                    lhsT=wc[:, t, g, :].bitcast(E4),
                    lhsT_scale=ws[:, t, g, :],
                    rhs=codes[:, win : win + 512].bitcast(E5),
                    rhs_scale=plane[:, win : win + 512],
                    start=(cm == 0),
                    stop=(cm == 3),
                )
            tiles[("az", q, t, s)] = a

        def evict_z(eng, q, t, s):
            k = ("oz", q, t)
            if k not in tiles:
                if (q, t) == (1, 1):
                    tiles[k] = work.tile([P, 2048], F32, name="oz%d_%d" % (t, q), tag="big", bufs=3)
                else:
                    tiles[k] = work.tile([P, 2048], F32, name="oz%d_%d" % (t, q), tag="oz", bufs=4)
            dst = tiles[k][:].rearrange("p (r4 rm c4 cm) -> p rm r4 c4 cm", r4=8, rm=4, c4=16, cm=4)[:, s]
            src = tiles[("az", q, t, s)][:].rearrange("p (cm r4 c4) -> p r4 c4 cm", cm=4, r4=8, c4=16)
            if eng == "V":
                nc.vector.tensor_copy(out=dst, in_=src)
            else:
                nc.scalar.copy(out=dst, in_=src)

        def store_z(q, t):
            ov = out[0].rearrange("(t p) r c -> t p (r c)", p=P)
            nc.sync.dma_start(out=ov[t][:, 2048 * q : 2048 * q + 2048], in_=tiles[("oz", q, t)][:])

        def passes_j(t, s):
            for cm in range(4):
                g = 4 * s + cm
                g0 = 4 * s + 2 * (cm // 2)
                a = psum.tile([P, 512], F32, name="aj%d_%d" % (t, g), tag="acc")
                nc.tensor.matmul_mx(
                    out=a[:],
                    lhsT=wc[:, t, g, :].bitcast(E4),
                    lhsT_scale=ws[:, t, g, :],
                    rhs=g1c[:, g0 : g0 + 2, :].rearrange("p g x -> p (g x)").bitcast(E5),
                    rhs_scale=g1s[:, g0 : g0 + 2, :].rearrange("p g x -> p (g x)"),
                    start=True,
                    stop=True,
                )
                tiles[("aj", t, s, cm)] = a

        def evict_j(eng, t, s, cm, x0, x1):
            k = ("ev", t, s)
            if k not in tiles:
                tiles[k] = work.tile([P, 4, 256], F32, name="ev%d_%d" % (t, s), tag="wv", bufs=3, align_bytes=64)
            lo = 256 * (cm % 2)
            if eng == "V":
                nc.vector.tensor_copy(out=tiles[k][:, cm, x0:x1], in_=tiles[("aj", t, s, cm)][:, lo + x0 : lo + x1])
            else:
                nc.scalar.copy(out=tiles[k][:, cm, x0:x1], in_=tiles[("aj", t, s, cm)][:, lo + x0 : lo + x1])

        def interleave_j(t, s, x0, x1):
            k = ("osb", t)
            if k not in tiles:
                tiles[k] = work.tile([P, 4096], F32, name="osb%d" % t, tag="big", bufs=3)
            dst = tiles[k][:].rearrange("p (r4 rm c i cm) -> p rm r4 c cm i", r4=16, rm=4, c=4, i=4, cm=4)[:, s, x0 // 16 : x1 // 16]
            src = tiles[("ev", t, s)][:].rearrange("p cm (r4 c i) -> p r4 c cm i", r4=16, c=4, i=4)[:, x0 // 16 : x1 // 16]
            nc.vector.tensor_copy(out=dst, in_=src)

        def store_j(t, x0, x1):
            ov = out[1].rearrange("(t p) r c -> t p (r c)", p=P)
            nc.sync.dma_start(out=ov[t][:, 16 * x0 : 16 * x1], in_=tiles[("osb", t)][:, 16 * x0 : 16 * x1])

        units = [(s, t) for s in range(4) for t in range(3)]
        stages = [(t, s) for t in range(3) for s in range(4)]

        def add(eng, tok):
            k = tok[0]
            if k == "zero":
                op("V", ("zero",), [], zeros)
            elif k == "rg":
                c, rm, h = tok[1], tok[2], tok[3]
                op(eng, ("rg", c, rm, h), [("ld", c, h)], lambda: regroup_g(eng, c, rm, h))
            elif k == "qz":
                q, rm = tok[1], tok[2]
                deps = [("rg", q, rm, h) for h in range(len(PIECES[q]))]
                if q == 1:
                    deps = deps + [("pz", 0, t, rm) for t in range(3)]
                op("V", ("qz", q, rm), deps, lambda: quant_z(q, rm))
            elif k == "qj":
                rm = tok[1]
                op("V", ("qj", rm), [("rg", 2, rm, 0), ("rg", 3, rm, 0)], lambda: quant_j(rm))
            elif k == "rw":
                s, t, h, c0, c1 = tok[1], tok[2], tok[3], tok[4], tok[5]
                g0, g1 = WPIECES[s][h]
                op(eng, ("rw", s, t, h, c0), [("ldw", s, h)], lambda: regroup_w(eng, s, t, g0, g1, c0, c1))
            elif k == "qw":
                s, t = tok[1], tok[2]
                deps = [("rw", s, t, h, 0) for h in range(len(WPIECES[s]))]
                if t == 1 and 0 < W1_CUT[s] < 32:
                    deps = deps + [("rw", s, t, h, W1_CUT[s]) for h in range(len(WPIECES[s]))]
                op("V", ("qw", s, t), deps, lambda: quant_w(s, t))
            elif k == "ez":
                q, t, s = tok[1], tok[2], tok[3]
                op(eng, ("ez", q, t, s), [("pz", q, t, s)], lambda: evict_z(eng, q, t, s))
            elif k == "ej":
                t, s, cm, x0, x1 = tok[1], tok[2], tok[3], tok[4], tok[5]
                op(eng, ("ej", t, s, cm, x0), [("pj", t, s)], lambda: evict_j(eng, t, s, cm, x0, x1))
            elif k == "ij":
                t, s, x0, x1 = tok[1], tok[2], tok[3], tok[4]
                op("V", ("ij", t, s, x0), [("ej", t, s, cm, x0) for cm in range(4)], lambda: interleave_j(t, s, x0, x1))
            elif k == "pz":
                q, t, s = tok[1], tok[2], tok[3]
                op("PE", ("pz", q, t, s), [("qw", s, t), ("qz", q, s)], lambda: passes_z(q, t, s))
            elif k == "pj":
                t, s = tok[1], tok[2]
                op("PE", ("pj", t, s), [("qw", s, t), ("qj", s)], lambda: passes_j(t, s))
            elif k == "ld":
                c, h = tok[1], tok[2]
                op("SP", ("ld", c, h), [], lambda: load_g(c, h))
            elif k == "ldw":
                s, h = tok[1], tok[2]
                g0, g1 = WPIECES[s][h]
                op("SP", ("ldw", s, h), [], lambda: load_w(s, g0, g1))
            elif k == "sz":
                q, t = tok[1], tok[2]
                op("SP", ("sz", q, t), [("ez", q, t, s) for s in range(4)], lambda: store_z(q, t))
            elif k == "sj":
                t, x0, x1 = tok[1], tok[2], tok[3]
                deps = [("ij", t, s, 0) for s in range(3)] + [("ij", t, 3, x0)]
                op("SP", ("sj", t, x0), deps, lambda: store_j(t, x0, x1))

        scripts = SCRIPTS(units, stages)
        for eng in ("SP", "V", "S", "PE"):
            for tok in scripts[eng]:
                add(eng, tok)

        done = set()
        heads = {"SP": 0, "V": 0, "S": 0, "PE": 0}
        left = sum(len(queues[e]) for e in queues)
        while left > 0:
            moved = 0
            for e in ("SP", "V", "S", "PE"):
                if heads[e] < len(queues[e]):
                    k = queues[e][heads[e]]
                    deps, fn = ops[k]
                    if all(d in done for d in deps):
                        fn()
                        done.add(k)
                        heads[e] = heads[e] + 1
                        moved = moved + 1
            assert moved > 0
            left = left - moved
